import numpy as np
import ml_dtypes


def mxq(x, axis, fmt="e4m3"):
    dtype, down = {"e4m3": (ml_dtypes.float8_e4m3fn, 7), "e5m2": (ml_dtypes.float8_e5m2, 14)}[fmt]
    v = np.moveaxis(np.asarray(x, np.float32).astype(ml_dtypes.bfloat16).astype(np.float64), axis, -1)
    blocks = v.reshape(v.shape[:-1] + (-1, 32))
    amax = np.abs(blocks).max(-1, keepdims=True)
    byte = np.maximum(np.where(amax > 0, np.frexp(amax)[1] - 1 + 127, 0) - down, 1)
    scale = np.exp2(byte - 127.0)
    codes = (blocks / scale).astype(np.float32).astype(dtype).astype(np.float64)
    return np.moveaxis((codes * scale).reshape(v.shape), -1, axis)


WIDE = False


def mx_kscale(k):
    if not WIDE:
        return np.ones(k)
    levels = np.array([10, -10, 5, -5, 0])
    if k % 512:
        return np.exp2(np.random.permutation(np.resize(levels, k // 32))).repeat(32)
    a = np.empty((k // 512, 16))
    for p in range(k // 512):
        a[p, :8] = np.random.permutation(np.resize(levels, 8))
        for g in range(8):
            far = levels[np.abs(levels - a[p, g]) >= 10]
            a[p, g + 8] = far[np.random.randint(len(far))]
    return np.exp2(a.ravel()).repeat(32)


BF16 = ml_dtypes.bfloat16


def bf(x):
    return np.asarray(x, np.float32).astype(BF16)


def f64(x):
    return np.asarray(x).astype(np.float64)


E2M1 = np.array([0.0, 0.5, 1.0, 1.5, 2.0, 3.0, 4.0, 6.0, -0.0, -0.5, -1.0, -1.5, -2.0, -3.0, -4.0, -6.0])


def pack_weight(w, fmt):
    k, n = w.shape
    w = f64(bf(w)).reshape(k // 32, 32, n)
    amax = np.abs(w).max(1)
    if fmt == "e4m3":
        byte = np.frexp(amax)[1] - 1 + 127 - 7
    else:
        mant, ex = np.frexp(amax / 6.0)
        byte = np.where(mant > 0.5, ex, ex - 1) + 127
    byte = np.clip(np.where(amax > 0, byte, 1), 1, 254)
    scaled = (w * np.exp2(127.0 - byte)[:, None, :]).reshape(k, n).astype(np.float32)
    by_word = np.ascontiguousarray(scaled.reshape(k // 512, 128, 4, n).transpose(0, 1, 3, 2))
    if fmt == "e4m3":
        words = by_word.astype(ml_dtypes.float8_e4m3fn).view(np.uint8)
    else:
        c = by_word.astype(ml_dtypes.float4_e2m1fn).view(np.uint8) & 0xF
        words = c[..., 0::2] | (c[..., 1::2] << 4)
    return np.ascontiguousarray(words), np.ascontiguousarray(byte.astype(np.uint8).reshape(k // 512, 16, n))


def unpack_weight(words, scales, fmt):
    g, p, n, _ = words.shape
    if fmt == "e4m3":
        vals = np.ascontiguousarray(words).view(ml_dtypes.float8_e4m3fn).astype(np.float64)
    else:
        nib = np.empty((g, p, n, 4), np.uint8)
        nib[..., 0::2] = words & 0xF
        nib[..., 1::2] = words >> 4
        vals = E2M1[nib]
    vals = vals * np.repeat(np.exp2(scales.astype(np.float64) - 127.0), 8, axis=1)[..., None]
    return vals.transpose(0, 1, 3, 2).reshape(g * 512, n)


N, E, G, M, H = 4096, 512, 512, 256, 1
HG = H * G


def sigmoid(v):
    return 1.0 / (1.0 + np.exp(-v))


def draw0():
    r = np.random.standard_normal
    s = mx_kscale(E)
    t = np.tile(mx_kscale(G), H)
    q = bf(r((N, E)) * s)
    rep = bf(r((N, E)) * s)
    Wq_words, Wq_scales = pack_weight(r((E, HG)) * G ** 0.25 / np.sqrt(E) / s[:, None], "e4m3")
    Wk_words, Wk_scales = pack_weight(r((E, HG)) * G ** 0.25 / np.sqrt(E) / s[:, None], "e4m3")
    Wv_words, Wv_scales = pack_weight(r((E, HG)) / np.sqrt(E) / s[:, None] * t, "e4m3")
    return {"q": q,
            "rep": rep,
            "Wq_words": Wq_words,
            "Wq_scales": Wq_scales,
            "Wk_words": Wk_words,
            "Wk_scales": Wk_scales,
            "Wv_words": Wv_words,
            "Wv_scales": Wv_scales,
            "W1": bf(r((H, G, M)) * 2.0 / np.sqrt(G) / t.reshape(H, G, 1)),
            "b1": bf(r((H, M)) * 0.2)}


def core(q, rep, Wq_words, Wq_scales, Wk_words, Wk_scales, Wv_words, Wv_scales, W1, b1):
    qq = mxq(f64(q), 1, "e4m3")
    rq = mxq(f64(rep), 1, "e4m3")
    Qh = (qq @ unpack_weight(Wq_words, Wq_scales, "e4m3")).reshape(N, H, G)
    Kh = (rq @ unpack_weight(Wk_words, Wk_scales, "e4m3")).reshape(N, H, G)
    Vh = (rq @ unpack_weight(Wv_words, Wv_scales, "e4m3")).reshape(N, H, G)
    gate = sigmoid(Qh * Kh * (1.0 / np.sqrt(G)))
    z = gate * Vh
    zt = z.transpose(1, 0, 2)
    pre = (mxq(zt, 2, "e4m3") @ mxq(f64(W1), 1, "e4m3")).transpose(1, 0, 2)
    return np.maximum(pre + f64(b1), 0.0)


def e4m3fn_bytes(y):
    return np.clip(np.asarray(y, np.float64), -448.0, 448.0).astype(np.float32).astype(ml_dtypes.float8_e4m3fn).view(np.uint8)


def e4m3fn_values(b):
    return np.asarray(b, np.uint8).view(ml_dtypes.float8_e4m3fn).astype(np.float64)


def setup_inputs():
    d = draw0()
    x0 = np.asarray(d['rep']).astype(np.float64)
    s = (np.max(np.abs(x0), axis=(0,), keepdims=True) / 448.0).astype(np.float32)
    out = {}
    for k, v in d.items():
        if k == 'rep':
            out['rep_bytes'] = e4m3fn_bytes(x0 / s.astype(np.float64))
            out['rep_scale'] = s
        else:
            out[k] = v
    return out


def reference(q, rep_bytes, rep_scale, Wq_words, Wq_scales, Wk_words, Wk_scales, Wv_words, Wv_scales, W1, b1):
    return core(q, e4m3fn_values(rep_bytes) * rep_scale.astype(np.float64), Wq_words, Wq_scales, Wk_words, Wk_scales, Wv_words, Wv_scales, W1, b1)

@@ -1,0 +1,357 @@
+from contextlib import ExitStack
+
+import concourse.mybir as mybir
+from concourse.masks import make_identity
+
+N, E, G, M = 4096, 512, 512, 256
+FLOPS = 2 * N * E * G * 3 + 2 * N * G * M
+
+F32 = mybir.dt.float32
+BF16 = mybir.dt.bfloat16
+I32 = mybir.dt.int32
+U32 = mybir.dt.uint32
+U8 = mybir.dt.uint8
+F8 = mybir.dt.float8_e4m3fn
+FP8X4 = mybir.dt.float8_e4m3fn_x4
+ACT = mybir.ActivationFunctionType
+ALU = mybir.AluOpType
+
+P = 128
+CHUNK = 512
+JB = 4
+BLOCKS = N // P
+CHUNKS = N // CHUNK
+GATE_SCALE = 1.0 / (512.0 ** 0.5)
+
+
+def tile_treehopnode_pa_t_w8_kernel(
+    tc, q, rep_bytes, rep_scale, Wq_words, Wq_scales, Wk_words, Wk_scales, Wv_words, Wv_scales, W1, b1, out
+):
+    nc = tc.nc
+    with ExitStack() as ctx:
+        keep = ctx.enter_context(tc.tile_pool(name="keep", bufs=1))
+        stage = ctx.enter_context(tc.tile_pool(name="stage", bufs=3))
+        psum = ctx.enter_context(tc.psum_pool(name="psum", bufs=1))
+
+        ident = keep.tile([P, P], F32, name="ident", align_bytes=64)
+        make_identity(nc, ident[:])
+        warm = keep.tile([P, 1], F32, name="warm")
+        nc.gpsimd.memset(warm[:], 0.0)
+        ctx.enter_context(tc.manual_schedule())
+
+        q_raw = [keep.tile([P, JB * E], BF16, name="q_raw%d" % c, align_bytes=64) for c in range(CHUNKS)]
+        r_raw = [keep.tile([P, JB * E], U8, name="r_raw%d" % c, align_bytes=64) for c in range(CHUNKS)]
+        scale_bc = keep.tile([P, E], F32, name="scale_bc", align_bytes=64)
+        w_raw = [keep.tile([P, G], I32, name="w_raw%d" % i, align_bytes=64) for i in range(3)]
+        w_codes = [keep.tile([P, G], I32, name="w_codes%d" % i, align_bytes=64) for i in range(3)]
+        ws_raw = keep.tile([P, G], U8, name="ws_raw", align_bytes=64)
+        ws = keep.tile([P, G], U8, name="ws", align_bytes=64)
+        w1_raw = keep.tile([P, JB, M], BF16, name="w1_raw", align_bytes=64)
+        w1_grp = keep.tile([P, M, JB], BF16, name="w1_grp", align_bytes=64)
+        w1_codes = keep.tile([P, M], U32, name="w1_codes", align_bytes=64)
+        w1_scales = keep.tile([P, M], U8, name="w1_scales", align_bytes=64)
+        b_col = [keep.tile([P, 1], BF16, name="b_col%d" % h, align_bytes=64) for h in range(2)]
+        b_bc = keep.tile([P, M], BF16, name="b_bc", align_bytes=64)
+
+        def rows(x, c):
+            return x[c * CHUNK : (c + 1) * CHUNK]
+
+        def load_q(c):
+            nc.sync.dma_start(out=q_raw[c][:], in_=rows(q, c).rearrange("(p j) k -> p (j k)", j=JB))
+
+        def load_r(c):
+            nc.sync.dma_start(out=r_raw[c][:], in_=rows(rep_bytes, c).rearrange("(p j) k -> p (j k)", j=JB))
+
+        words = (Wq_words, Wk_words, Wv_words)
+        scales = (Wq_scales, Wk_scales, Wv_scales)
+
+        def load_w(i):
+            nc.sync.dma_start(out=w_raw[i][:], in_=words[i][0].rearrange("p n t -> p (n t)").bitcast(I32))
+
+        nc.vector.memset(ws_raw[:].bitcast(I32), 0)
+        nc.scalar.dma_start(out=scale_bc[:], in_=rep_scale.rearrange("o k -> (o k)").partition_broadcast(P))
+        load_r(0)
+        load_q(0)
+        load_w(1)
+        for i in (1, 0, 2):
+            for quad in range(4):
+                lo = 32 * quad + 4 * i
+                nc.sync.dma_start(
+                    out=ws_raw[lo : lo + 4, :].bitcast(I32), in_=scales[i][0, 4 * quad : 4 * quad + 4, :].bitcast(I32)
+                )
+        load_w(0)
+        load_w(2)
+        load_r(1)
+        load_q(1)
+        nc.sync.dma_start(out=w1_raw[:], in_=W1[0].rearrange("(p j) m -> p j m", j=JB))
+        with nc.allow_non_contiguous_dma(reason="one bias value to a partition, 256 in all"):
+            for h in range(2):
+                nc.scalar.dma_start(
+                    out=b_col[h][:], in_=b1[:, h * P : (h + 1) * P].rearrange("o p -> p o")
+                )
+        nc.scalar.dma_start(out=b_bc[:], in_=b1.rearrange("o m -> (o m)").partition_broadcast(P))
+        nc.scalar.activation(out=warm[:], in_=warm[:], func=ACT.Sigmoid)
+        for c in range(2, CHUNKS):
+            load_r(c)
+            load_q(c)
+
+        r_bf, r_bank, q_bank, r_grp, q_grp = {}, {}, {}, {}, {}
+        r_codes, r_scales, q_codes, q_scales = {}, {}, {}, {}
+        k_bank, q_acc, v_bank, k_sb, gate, z_grp, z_codes, z_scales = {}, {}, {}, {}, {}, {}, {}, {}
+        o_bank, o_sb, t_bank, res = {}, {}, {}, {}
+
+        def permute_w(i):
+            nc.vector.tensor_copy(
+                out=w_codes[i][:].rearrange("p (t m) -> p t m", t=4), in_=w_raw[i][:].rearrange("p (m t) -> p t m", t=4)
+            )
+
+        def permute_scales():
+            nc.vector.tensor_copy(
+                out=ws[:].rearrange("p (t m) -> p t m", t=4), in_=ws_raw[:].rearrange("p (m t) -> p t m", t=4)
+            )
+
+        def prod(b):
+            if not 0 <= b < BLOCKS:
+                return
+            h, i = b // 2, b % 2
+            if i == 0:
+                r_bf[h] = stage.tile([P, 2 * E], BF16, name="r_bf", align_bytes=64)
+            j = b % JB
+            nc.vector.tensor_tensor(
+                out=r_bf[h][:, i * E : (i + 1) * E],
+                in0=r_raw[b // JB][:, j * E : (j + 1) * E].bitcast(F8),
+                in1=scale_bc[:],
+                op=ALU.mult,
+            )
+
+        def transposes(b0):
+            if not 0 <= b0 < BLOCKS:
+                return
+            h = b0 // 2
+            r_bank[h] = psum.tile([P, 2, 2, P], F32, name="r_bank")
+            q_bank[h] = psum.tile([P, 2, 2, P], F32, name="q_bank")
+            rw = r_bf[h][:].bitcast(F32)
+            qw = q_raw[b0 // JB][:].bitcast(F32)
+            qoff = (b0 % JB) * (E // 2)
+            for bank, w, off in ((r_bank[h], rw, 0), (q_bank[h], qw, qoff)):
+                for i in range(2):
+                    for u in range(2):
+                        lo = off + i * (E // 2)
+                        nc.tensor.transpose(bank[:, i, u, :], w[:, lo + u : lo + E // 2 : 2], ident[:])
+
+        def evac(bank, tag):
+            grp = stage.tile([P, 2 * P * 4], BF16, name=tag, align_bytes=64)
+            nc.scalar.copy(
+                out=grp[:].bitcast(F32).rearrange("p (i r u) -> p i r u", i=2, u=2),
+                in_=bank[:].rearrange("p i u r -> p i r u"),
+            )
+            return grp
+
+        def evac_r(b0):
+            if 0 <= b0 < BLOCKS:
+                r_grp[b0 // 2] = evac(r_bank[b0 // 2], "r_grp")
+
+        def evac_q(b0):
+            if 0 <= b0 < BLOCKS:
+                q_grp[b0 // 2] = evac(q_bank[b0 // 2], "q_grp")
+
+        def quant(grp, cols, tag):
+            codes = stage.tile([P, cols], U32, name=tag + "_codes", align_bytes=64)
+            sc = stage.tile([P, cols], U8, name=tag + "_scales", align_bytes=64)
+            nc.vector.quantize_mx(out=codes[:].bitcast(FP8X4), scales=sc[:], in_=grp)
+            return codes, sc
+
+        def quant_r(b0):
+            if 0 <= b0 < BLOCKS:
+                h = b0 // 2
+                r_codes[h], r_scales[h] = quant(r_grp[h][:], 2 * P, "r")
+
+        def quant_q(b0):
+            if 0 <= b0 < BLOCKS:
+                h = b0 // 2
+                q_codes[h], q_scales[h] = quant(q_grp[h][:], 2 * P, "q")
+
+        def project(bank, i, codes, sc, b):
+            cols = slice((b % 2) * P, (b % 2 + 1) * P)
+            for t in range(4):
+                wc = slice(t * P, (t + 1) * P)
+                nc.tensor.matmul_mx(
+                    out=bank[:, t, :],
+                    lhsT=w_codes[i][:, wc].bitcast(FP8X4),
+                    lhsT_scale=ws[4 * i : P, wc],
+                    rhs=codes[:, cols].bitcast(FP8X4),
+                    rhs_scale=sc[:, cols],
+                    start=True,
+                    stop=True,
+                )
+
+        def mm_q(b):
+            if 0 <= b < BLOCKS:
+                q_acc[b] = psum.tile([P, 4, P], F32, name="q_acc")
+                project(q_acc[b], 0, q_codes[b // 2], q_scales[b // 2], b)
+
+        def mm_k(b):
+            if 0 <= b < BLOCKS:
+                k_bank[b] = psum.tile([P, 4, P], F32, name="k_bank")
+                project(k_bank[b], 1, r_codes[b // 2], r_scales[b // 2], b)
+
+        def mm_v(b):
+            if 0 <= b < BLOCKS:
+                v_bank[b] = psum.tile([P, 4, P], F32, name="v_bank", bufs=2)
+                project(v_bank[b], 2, r_codes[b // 2], r_scales[b // 2], b)
+
+        def copy_k(b):
+            if 0 <= b < BLOCKS:
+                k_sb[b] = stage.tile([P, P, 4], F32, name="k_sb", align_bytes=64)
+                nc.scalar.copy(out=k_sb[b][:], in_=k_bank[b][:].rearrange("p t n -> p n t"))
+
+        def mul_qk(b):
+            if 0 <= b < BLOCKS:
+                gate[b] = stage.tile([P, P, 4], F32, name="gate", align_bytes=64)
+                nc.vector.tensor_tensor(
+                    out=gate[b][:], in0=q_acc[b][:].rearrange("p t n -> p n t"), in1=k_sb[b][:], op=ALU.mult
+                )
+
+        def sigmoid(b):
+            if 0 <= b < BLOCKS:
+                k_sb[b] = stage.tile([P, P, 4], F32, name="sig", align_bytes=64)
+                nc.scalar.activation(out=k_sb[b][:], in_=gate[b][:], func=ACT.Sigmoid, scale=GATE_SCALE)
+
+        def mul_v(b):
+            if 0 <= b < BLOCKS:
+                c, j = b // JB, b % JB
+                if j == 0:
+                    z_grp[c] = stage.tile([P, CHUNK, 4], BF16, name="z_grp", align_bytes=64, bufs=2)
+                nc.vector.tensor_tensor(
+                    out=z_grp[c][:, j * P : (j + 1) * P, :],
+                    in0=v_bank[b][:].rearrange("p t n -> p n t"),
+                    in1=k_sb[b][:],
+                    op=ALU.mult,
+                )
+
+        def quant_z(c):
+            if 0 <= c < CHUNKS - 1:
+                z_codes[c], z_scales[c] = quant(z_grp[c][:].rearrange("p n t -> p (n t)"), CHUNK, "z")
+
+        def layer(c):
+            if 0 <= c < CHUNKS - 1:
+                for h in range(2):
+                    o_bank[c, h] = psum.tile([P, CHUNK], F32, name="o_bank%d" % h)
+                    wc = slice(h * P, (h + 1) * P)
+                    nc.tensor.matmul_mx(
+                        out=o_bank[c, h][:],
+                        lhsT=w1_codes[:, wc].bitcast(FP8X4),
+                        lhsT_scale=w1_scales[:, wc],
+                        rhs=z_codes[c][:].bitcast(FP8X4),
+                        rhs_scale=z_scales[c][:],
+                        start=True,
+                        stop=True,
+                    )
+
+        def relu(c, h):
+            if 0 <= c < CHUNKS - 1:
+                o_sb[c, h] = stage.tile([P, CHUNK], F32, name="o_sb%d" % h, align_bytes=64, bufs=2)
+                nc.scalar.activation(
+                    out=o_sb[c, h][:], in_=o_bank[c, h][:], func=ACT.Relu, bias=b_col[h][:]
+                )
+
+        def turn(c):
+            if 0 <= c < CHUNKS - 1:
+                for half in range(2):
+                    t_bank[c, half] = psum.tile([P, 2, M], F32, name="o_bank%d" % half)
+                    for jj in range(2):
+                        j = 2 * half + jj
+                        for h in range(2):
+                            nc.tensor.transpose(
+                                t_bank[c, half][:, jj, h * P : (h + 1) * P], o_sb[c, h][:, j * P : (j + 1) * P], ident[:]
+                            )
+
+        def finish(c, half):
+            if 0 <= c < CHUNKS - 1:
+                if half == 0:
+                    res[c] = stage.tile([P, JB, M], F32, name="res", align_bytes=64, bufs=2)
+                nc.scalar.copy(out=res[c][:, 2 * half : 2 * half + 2, :], in_=t_bank[c, half][:])
+                if half == 1:
+                    nc.sync.dma_start(out=rows(out, c).rearrange("(p j) o m -> p j (o m)", j=JB), in_=res[c][:])
+
+        last = CHUNKS - 1
+
+        def last_quant(b):
+            if last * JB <= b < BLOCKS:
+                j = b % JB
+                z_codes[b, 0], z_scales[b, 0] = quant(
+                    z_grp[last][:, j * P : (j + 1) * P, :].rearrange("p n t -> p (n t)"), P, "zl"
+                )
+                o_bank[b, 2] = psum.tile([P, M], F32, name="q_bank" if b % 2 else "r_bank")
+                nc.tensor.matmul_mx(
+                    out=o_bank[b, 2][:],
+                    lhsT=z_codes[b, 0][:].bitcast(FP8X4),
+                    lhsT_scale=z_scales[b, 0][:],
+                    rhs=w1_codes[:].bitcast(FP8X4),
+                    rhs_scale=w1_scales[:],
+                    start=True,
+                    stop=True,
+                )
+
+        def last_out(b):
+            if last * JB <= b < BLOCKS:
+                j = b % JB
+                pre = stage.tile([P, M], F32, name="pre", align_bytes=64)
+                act = stage.tile([P, M], F32, name="act", align_bytes=64)
+                nc.vector.tensor_tensor(out=pre[:], in0=o_bank[b, 2][:], in1=b_bc[:], op=ALU.add)
+                nc.scalar.activation(out=act[:], in_=pre[:], func=ACT.Relu)
+                nc.sync.dma_start(
+                    out=rows(out, last).rearrange("(p j) o m -> p j (o m)", j=JB)[:, j, :], in_=act[:]
+                )
+
+        for s in range(-5, BLOCKS + 5):
+            m4 = s % 4
+            even = s % 2 == 0
+            mm_v(s)
+            mul_qk(s)
+            copy_k(s + 1)
+            if not even:
+                transposes(s + 3)
+            if m4 == 2:
+                layer((s - 6) // 4)
+            if m4 == 0:
+                turn((s - 8) // 4)
+            if even:
+                if s == -2:
+                    permute_w(1)
+                    permute_scales()
+                quant_r(s + 2)
+            else:
+                if m4 == 1:
+                    quant_z((s - 5) // 4)
+                prod(s + 5)
+            if even:
+                evac_q(s + 2)
+            elif m4 == 3:
+                relu((s - 7) // 4, 1)
+            else:
+                finish((s - 9) // 4, 1)
+            mul_v(s - 1)
+            sigmoid(s)
+            if even:
+                prod(s + 5)
+                quant_q(s + 2)
+            if s == -2:
+                permute_w(0)
+            if s == -1:
+                permute_w(2)
+                nc.scalar.copy(out=w1_grp[:], in_=w1_raw[:].rearrange("p j m -> p m j"))
+            if s == 1:
+                nc.vector.quantize_mx(
+                    out=w1_codes[:].bitcast(FP8X4), scales=w1_scales[:], in_=w1_grp[:].rearrange("p m j -> p (m j)")
+                )
+            if not even:
+                evac_r(s + 3)
+            elif m4 == 2:
+                relu((s - 6) // 4, 0)
+            else:
+                finish((s - 8) // 4, 0)
+            last_out(s - 3)
+            last_quant(s - 2)
+            mm_k(s + 2)
+            mm_q(s + 1)

@@ -21,6 +21,7 @@ CHUNK = 512
 JB = 4
 BLOCKS = N // P
 CHUNKS = N // CHUNK
+E2_CHUNKS = CHUNKS - 2
 GATE_SCALE = 1.0 / (512.0 ** 0.5)
 
 
@@ -51,7 +52,7 @@ def tile_treehopnode_pa_t_w8_kernel(
         w1_codes = keep.tile([P, M], U32, name="w1_codes", align_bytes=64)
         w1_scales = keep.tile([P, M], U8, name="w1_scales", align_bytes=64)
         b_col = [keep.tile([P, 1], BF16, name="b_col%d" % h, align_bytes=64) for h in range(2)]
-        b_bc = keep.tile([P, M], BF16, name="b_bc", align_bytes=64)
+        b_bc = keep.tile([P, 2, M], BF16, name="b_bc", align_bytes=64)
 
         def rows(x, c):
             return x[c * CHUNK : (c + 1) * CHUNK]
@@ -68,11 +69,17 @@ def tile_treehopnode_pa_t_w8_kernel(
         def load_w(i):
             nc.sync.dma_start(out=w_raw[i][:], in_=words[i][0].rearrange("p n t -> p (n t)").bitcast(I32))
 
+        def load_part(c, j0, j1, raw, x):
+            nc.sync.dma_start(
+                out=raw[c][:, j0 * E : j1 * E],
+                in_=rows(x, c).rearrange("(p j) k -> p j k", j=JB)[:, j0:j1, :].rearrange("p j k -> p (j k)"),
+            )
+
         nc.vector.memset(ws_raw[:].bitcast(I32), 0)
         nc.scalar.dma_start(out=scale_bc[:], in_=rep_scale.rearrange("o k -> (o k)").partition_broadcast(P))
-        load_r(0)
-        load_q(0)
         load_w(1)
+        load_r(0)
+        load_part(0, 0, 2, q_raw, q)
         for i in (1, 0, 2):
             for quad in range(4):
                 lo = 32 * quad + 4 * i
@@ -80,20 +87,20 @@ def tile_treehopnode_pa_t_w8_kernel(
                     out=ws_raw[lo : lo + 4, :].bitcast(I32), in_=scales[i][0, 4 * quad : 4 * quad + 4, :].bitcast(I32)
                 )
         load_w(0)
+        load_part(0, 2, 4, q_raw, q)
         load_w(2)
         load_r(1)
         load_q(1)
         nc.sync.dma_start(out=w1_raw[:], in_=W1[0].rearrange("(p j) m -> p j m", j=JB))
-        with nc.allow_non_contiguous_dma(reason="one bias value to a partition, 256 in all"):
-            for h in range(2):
-                nc.scalar.dma_start(
-                    out=b_col[h][:], in_=b1[:, h * P : (h + 1) * P].rearrange("o p -> p o")
-                )
-        nc.scalar.dma_start(out=b_bc[:], in_=b1.rearrange("o m -> (o m)").partition_broadcast(P))
         nc.scalar.activation(out=warm[:], in_=warm[:], func=ACT.Sigmoid)
         for c in range(2, CHUNKS):
             load_r(c)
             load_q(c)
+            if c == 2:
+                with nc.allow_non_contiguous_dma(reason="one bias value to a partition, 256 in all"):
+                    for h in range(2):
+                        nc.sync.dma_start(out=b_col[h][:], in_=b1[:, h * P : (h + 1) * P].rearrange("o p -> p o"))
+        nc.sync.dma_start(out=b_bc[:, 0, :], in_=b1.rearrange("o m -> (o m)").partition_broadcast(P))
 
         r_bf, r_bank, q_bank, r_grp, q_grp = {}, {}, {}, {}, {}
         r_codes, r_scales, q_codes, q_scales = {}, {}, {}, {}
@@ -138,6 +145,44 @@ def tile_treehopnode_pa_t_w8_kernel(
                     for u in range(2):
                         lo = off + i * (E // 2)
                         nc.tensor.transpose(bank[:, i, u, :], w[:, lo + u : lo + E // 2 : 2], ident[:])
+
+        def head_half():
+            r_bank[0] = psum.tile([P, 2, 2, P], F32, name="r_bank")
+            q_bank[0] = psum.tile([P, 2, 2, P], F32, name="q_bank")
+            qw = q_raw[0][:].bitcast(F32)
+            for i in range(2):
+                for u in range(2):
+                    lo = i * (E // 2)
+                    nc.tensor.transpose(q_bank[0][:, i, u, :], qw[:, lo + u : lo + E // 2 : 2], ident[:])
+            evac_q(0)
+            permute_w(1)
+            r_grp[0] = stage.tile([P, 2 * P * 4], BF16, name="r_grp", align_bytes=64)
+            r_codes[0] = stage.tile([P, 2 * P], U32, name="r_codes", align_bytes=64)
+            r_scales[0] = stage.tile([P, 2 * P], U8, name="r_scales", align_bytes=64)
+            for i in range(2):
+                prod(i)
+                rw = r_bf[0][:].bitcast(F32)
+                lo = i * (E // 2)
+                for u in range(2):
+                    nc.tensor.transpose(r_bank[0][:, i, u, :], rw[:, lo + u : lo + E // 2 : 2], ident[:])
+                nc.scalar.copy(
+                    out=r_grp[0][:, i * E : (i + 1) * E].bitcast(F32).rearrange("p (r u) -> p r u", u=2),
+                    in_=r_bank[0][:, i].rearrange("p u r -> p r u"),
+                )
+            prod(2)
+            permute_scales()
+            for i in range(2):
+                nc.vector.quantize_mx(
+                    out=r_codes[0][:, i * P : (i + 1) * P].bitcast(FP8X4),
+                    scales=r_scales[0][:, i * P : (i + 1) * P],
+                    in_=r_grp[0][:, i * E : (i + 1) * E],
+                )
+                if i == 0:
+                    quant_q(0)
+                    permute_w(0)
+                    prod(3)
+            mm_k(0)
+            mm_q(0)
 
         def evac(bank, tag):
             grp = stage.tile([P, 2 * P * 4], BF16, name=tag, align_bytes=64)
@@ -230,11 +275,11 @@ def tile_treehopnode_pa_t_w8_kernel(
                 )
 
         def quant_z(c):
-            if 0 <= c < CHUNKS - 1:
+            if 0 <= c < E2_CHUNKS:
                 z_codes[c], z_scales[c] = quant(z_grp[c][:].rearrange("p n t -> p (n t)"), CHUNK, "z")
 
         def layer(c):
-            if 0 <= c < CHUNKS - 1:
+            if 0 <= c < E2_CHUNKS:
                 for h in range(2):
                     o_bank[c, h] = psum.tile([P, CHUNK], F32, name="o_bank%d" % h)
                     wc = slice(h * P, (h + 1) * P)
@@ -249,14 +294,14 @@ def tile_treehopnode_pa_t_w8_kernel(
                     )
 
         def relu(c, h):
-            if 0 <= c < CHUNKS - 1:
+            if 0 <= c < E2_CHUNKS:
                 o_sb[c, h] = stage.tile([P, CHUNK], F32, name="o_sb%d" % h, align_bytes=64, bufs=2)
                 nc.scalar.activation(
                     out=o_sb[c, h][:], in_=o_bank[c, h][:], func=ACT.Relu, bias=b_col[h][:]
                 )
 
         def turn(c):
-            if 0 <= c < CHUNKS - 1:
+            if 0 <= c < E2_CHUNKS:
                 for half in range(2):
                     t_bank[c, half] = psum.tile([P, 2, M], F32, name="o_bank%d" % half)
                     for jj in range(2):
@@ -267,44 +312,47 @@ def tile_treehopnode_pa_t_w8_kernel(
                             )
 
         def finish(c, half):
-            if 0 <= c < CHUNKS - 1:
+            if 0 <= c < E2_CHUNKS:
                 if half == 0:
                     res[c] = stage.tile([P, JB, M], F32, name="res", align_bytes=64, bufs=2)
                 nc.scalar.copy(out=res[c][:, 2 * half : 2 * half + 2, :], in_=t_bank[c, half][:])
                 if half == 1:
                     nc.sync.dma_start(out=rows(out, c).rearrange("(p j) o m -> p j (o m)", j=JB), in_=res[c][:])
 
-        last = CHUNKS - 1
+        def tail_quant(b, n):
+            c, j = b // JB, b % JB
+            z_codes[b, 0], z_scales[b, 0] = quant(
+                z_grp[c][:, j * P : (j + n) * P, :].rearrange("p n t -> p (n t)"), n * P, "zl%d" % n
+            )
 
-        def last_quant(b):
-            if last * JB <= b < BLOCKS:
-                j = b % JB
-                z_codes[b, 0], z_scales[b, 0] = quant(
-                    z_grp[last][:, j * P : (j + 1) * P, :].rearrange("p n t -> p (n t)"), P, "zl"
-                )
-                o_bank[b, 2] = psum.tile([P, M], F32, name="q_bank" if b % 2 else "r_bank")
+        def tail_layer(b, n, tag):
+            o_bank[b, 2] = psum.tile([P, n, M], F32, name=tag)
+            for i in range(n):
+                cols = slice(i * P, (i + 1) * P)
                 nc.tensor.matmul_mx(
-                    out=o_bank[b, 2][:],
-                    lhsT=z_codes[b, 0][:].bitcast(FP8X4),
-                    lhsT_scale=z_scales[b, 0][:],
+                    out=o_bank[b, 2][:, i, :],
+                    lhsT=z_codes[b, 0][:, cols].bitcast(FP8X4),
+                    lhsT_scale=z_scales[b, 0][:, cols],
                     rhs=w1_codes[:].bitcast(FP8X4),
                     rhs_scale=w1_scales[:],
                     start=True,
                     stop=True,
                 )
 
-        def last_out(b):
-            if last * JB <= b < BLOCKS:
-                j = b % JB
-                pre = stage.tile([P, M], F32, name="pre", align_bytes=64)
-                act = stage.tile([P, M], F32, name="act", align_bytes=64)
-                nc.vector.tensor_tensor(out=pre[:], in0=o_bank[b, 2][:], in1=b_bc[:], op=ALU.add)
-                nc.scalar.activation(out=act[:], in_=pre[:], func=ACT.Relu)
-                nc.sync.dma_start(
-                    out=rows(out, last).rearrange("(p j) o m -> p j (o m)", j=JB)[:, j, :], in_=act[:]
-                )
+        def tail_add(b, n):
+            res[b, 0] = stage.tile([P, n, M], F32, name="pre%d" % n, align_bytes=64)
+            nc.vector.tensor_tensor(out=res[b, 0][:], in0=o_bank[b, 2][:], in1=b_bc[:, 0:n, :], op=ALU.add)
 
-        for s in range(-5, BLOCKS + 5):
+        def tail_relu(b, n):
+            res[b, 1] = stage.tile([P, n, M], F32, name="post%d" % n, align_bytes=64)
+            nc.scalar.activation(out=res[b, 1][:], in_=res[b, 0][:], func=ACT.Relu)
+            j = b % JB
+            nc.sync.dma_start(
+                out=rows(out, b // JB).rearrange("(p j) o m -> p j (o m)", j=JB)[:, j : j + n, :], in_=res[b, 1][:]
+            )
+
+        head_half()
+        for s in range(-1, BLOCKS + 3):
             m4 = s % 4
             even = s % 2 == 0
             mm_v(s)
@@ -316,32 +364,59 @@ def tile_treehopnode_pa_t_w8_kernel(
                 layer((s - 6) // 4)
             if m4 == 0:
                 turn((s - 8) // 4)
+            if s == 27:
+                tail_quant(24, 2)
+            if s == 29:
+                tail_quant(26, 2)
+                tail_layer(26, 2, "q_bank")
+                tail_add(24, 2)
+            if s == 31:
+                tail_quant(28, 2)
+                tail_layer(28, 2, "r_bank")
+            if s == 32:
+                tail_add(28, 2)
             if even:
-                if s == -2:
-                    permute_w(1)
-                    permute_scales()
                 quant_r(s + 2)
             else:
                 if m4 == 1:
                     quant_z((s - 5) // 4)
-                prod(s + 5)
+                if s > -1:
+                    prod(s + 5)
             if even:
                 evac_q(s + 2)
             elif m4 == 3:
                 relu((s - 7) // 4, 1)
             else:
                 finish((s - 9) // 4, 1)
+            if s == 28:
+                tail_layer(24, 2, "r_bank")
+            if s == 30:
+                tail_relu(24, 2)
+                tail_add(26, 2)
+            if s == 31:
+                tail_relu(26, 2)
             mul_v(s - 1)
             sigmoid(s)
+            if s == 32:
+                tail_relu(28, 2)
+            if s in (31, 32):
+                tail_quant(s - 1, 1)
+                tail_layer(s - 1, 1, "o_bank%d" % (s % 2))
+            if s in (32, 33):
+                tail_add(s - 2, 1)
+                tail_relu(s - 2, 1)
             if even:
+                if s == 0:
+                    prod(4)
                 prod(s + 5)
                 quant_q(s + 2)
-            if s == -2:
-                permute_w(0)
             if s == -1:
                 permute_w(2)
+            if s == 2:
                 nc.scalar.copy(out=w1_grp[:], in_=w1_raw[:].rearrange("p j m -> p m j"))
-            if s == 1:
+            if s == 25:
+                nc.scalar.copy(out=b_bc[:, 1, :], in_=b_bc[:, 0, :])
+            if s == 4:
                 nc.vector.quantize_mx(
                     out=w1_codes[:].bitcast(FP8X4), scales=w1_scales[:], in_=w1_grp[:].rearrange("p m j -> p (m j)")
                 )
@@ -351,7 +426,6 @@ def tile_treehopnode_pa_t_w8_kernel(
                 relu((s - 6) // 4, 0)
             else:
                 finish((s - 8) // 4, 0)
-            last_out(s - 3)
-            last_quant(s - 2)
+            if s > -1:
+                mm_q(s + 1)
             mm_k(s + 2)
-            mm_q(s + 1)

@@ -43,6 +43,7 @@ def tile_treehopnode_pa_t_w8_kernel(
         q_raw = [keep.tile([P, JB * E], BF16, name="q_raw%d" % c, align_bytes=64) for c in range(CHUNKS)]
         r_raw = [keep.tile([P, JB * E], U8, name="r_raw%d" % c, align_bytes=64) for c in range(CHUNKS)]
         scale_bc = keep.tile([P, E], F32, name="scale_bc", align_bytes=64)
+        scale_col = keep.tile([P, 4], F32, name="scale_col", align_bytes=64)
         w_raw = [keep.tile([P, G], I32, name="w_raw%d" % i, align_bytes=64) for i in range(3)]
         w_codes = [keep.tile([P, G], I32, name="w_codes%d" % i, align_bytes=64) for i in range(3)]
         ws_raw = keep.tile([P, G], U8, name="ws_raw", align_bytes=64)
@@ -76,23 +77,27 @@ def tile_treehopnode_pa_t_w8_kernel(
             )
 
         nc.vector.memset(ws_raw[:].bitcast(I32), 0)
-        nc.scalar.dma_start(out=scale_bc[:], in_=rep_scale.rearrange("o k -> (o k)").partition_broadcast(P))
-        load_w(1)
-        load_r(0)
-        load_part(0, 0, 2, q_raw, q)
+        nc.scalar.dma_start(out=scale_col[:], in_=rep_scale.rearrange("o (p t) -> p (o t)", t=4))
+        scale_bank = psum.tile([P, 4, P], F32, name="k_bank")
+        for t in range(4):
+            nc.tensor.transpose(scale_bank[:, t, :], scale_col[:, t : t + 1].to_broadcast([P, P]), ident[:])
+        nc.scalar.activation(out=warm[:], in_=warm[:], func=ACT.Sigmoid)
+        nc.scalar.copy(out=scale_bc[:].rearrange("p (n t) -> p n t", t=4), in_=scale_bank[:].rearrange("p t n -> p n t"))
         for i in (1, 0, 2):
             for quad in range(4):
                 lo = 32 * quad + 4 * i
                 nc.sync.dma_start(
                     out=ws_raw[lo : lo + 4, :].bitcast(I32), in_=scales[i][0, 4 * quad : 4 * quad + 4, :].bitcast(I32)
                 )
+        load_r(0)
+        nc.sync.dma_start(out=w1_raw[:], in_=W1[0].rearrange("(p j) m -> p j m", j=JB))
+        load_part(0, 0, 2, q_raw, q)
+        load_w(1)
         load_w(0)
         load_part(0, 2, 4, q_raw, q)
         load_w(2)
         load_r(1)
         load_q(1)
-        nc.sync.dma_start(out=w1_raw[:], in_=W1[0].rearrange("(p j) m -> p j m", j=JB))
-        nc.scalar.activation(out=warm[:], in_=warm[:], func=ACT.Sigmoid)
         for c in range(2, CHUNKS):
             load_r(c)
             load_q(c)
@@ -155,7 +160,6 @@ def tile_treehopnode_pa_t_w8_kernel(
                     lo = i * (E // 2)
                     nc.tensor.transpose(q_bank[0][:, i, u, :], qw[:, lo + u : lo + E // 2 : 2], ident[:])
             evac_q(0)
-            permute_w(1)
             r_grp[0] = stage.tile([P, 2 * P * 4], BF16, name="r_grp", align_bytes=64)
             r_codes[0] = stage.tile([P, 2 * P], U32, name="r_codes", align_bytes=64)
             r_scales[0] = stage.tile([P, 2 * P], U8, name="r_scales", align_bytes=64)
@@ -169,8 +173,9 @@ def tile_treehopnode_pa_t_w8_kernel(
                     out=r_grp[0][:, i * E : (i + 1) * E].bitcast(F32).rearrange("p (r u) -> p r u", u=2),
                     in_=r_bank[0][:, i].rearrange("p u r -> p r u"),
                 )
-            prod(2)
             permute_scales()
+            permute_w(1)
+            prod(2)
             for i in range(2):
                 nc.vector.quantize_mx(
                     out=r_codes[0][:, i * P : (i + 1) * P].bitcast(FP8X4),
@@ -351,6 +356,7 @@ def tile_treehopnode_pa_t_w8_kernel(
                 out=rows(out, b // JB).rearrange("(p j) o m -> p j (o m)", j=JB)[:, j : j + n, :], in_=res[b, 1][:]
             )
 
+        nc.scalar.copy(out=w1_grp[:], in_=w1_raw[:].rearrange("p j m -> p m j"))
         head_half()
         for s in range(-1, BLOCKS + 3):
             m4 = s % 4
@@ -412,8 +418,6 @@ def tile_treehopnode_pa_t_w8_kernel(
                 quant_q(s + 2)
             if s == -1:
                 permute_w(2)
-            if s == 2:
-                nc.scalar.copy(out=w1_grp[:], in_=w1_raw[:].rearrange("p j m -> p m j"))
             if s == 25:
                 nc.scalar.copy(out=b_bc[:, 1, :], in_=b_bc[:, 0, :])
             if s == 4:

@@ -14,15 +14,27 @@ U8 = mybir.dt.uint8
 F8 = mybir.dt.float8_e4m3fn
 FP8X4 = mybir.dt.float8_e4m3fn_x4
 ACT = mybir.ActivationFunctionType
-ALU = mybir.AluOpType
+MULT = mybir.AluOpType.mult
+ADD = mybir.AluOpType.add
 
 P = 128
+PACK = 4
+WORDS = E // 2
 CHUNK = 512
-JB = 4
+JB = CHUNK // P
 BLOCKS = N // P
 CHUNKS = N // CHUNK
-E2_CHUNKS = CHUNKS - 2
-GATE_SCALE = 1.0 / (512.0 ** 0.5)
+HALVES = M // P
+GATE_SCALE = 1.0 / G**0.5
+
+CHANNEL_CHUNKS = CHUNKS - 2
+TOKEN_BLOCK = CHANNEL_CHUNKS * JB
+
+TOKEN_PAIRS = (
+    (TOKEN_BLOCK, "r_bank", 27, 28, 29, 30),
+    (TOKEN_BLOCK + 2, "q_bank", 29, 29, 30, 31),
+    (TOKEN_BLOCK + 4, "r_bank", 31, 31, 32, 32),
+)
 
 
 def tile_treehopnode_pa_t_w8_kernel(
@@ -38,398 +50,347 @@ def tile_treehopnode_pa_t_w8_kernel(
         make_identity(nc, ident[:])
         warm = keep.tile([P, 1], F32, name="warm")
         nc.gpsimd.memset(warm[:], 0.0)
-        ctx.enter_context(tc.manual_schedule())
 
         q_raw = [keep.tile([P, JB * E], BF16, name="q_raw%d" % c, align_bytes=64) for c in range(CHUNKS)]
         r_raw = [keep.tile([P, JB * E], U8, name="r_raw%d" % c, align_bytes=64) for c in range(CHUNKS)]
+        scale_col = keep.tile([P, PACK], F32, name="scale_col", align_bytes=64)
         scale_bc = keep.tile([P, E], F32, name="scale_bc", align_bytes=64)
-        scale_col = keep.tile([P, 4], F32, name="scale_col", align_bytes=64)
         w_raw = [keep.tile([P, G], I32, name="w_raw%d" % i, align_bytes=64) for i in range(3)]
         w_codes = [keep.tile([P, G], I32, name="w_codes%d" % i, align_bytes=64) for i in range(3)]
         ws_raw = keep.tile([P, G], U8, name="ws_raw", align_bytes=64)
         ws = keep.tile([P, G], U8, name="ws", align_bytes=64)
-        w1_raw = keep.tile([P, JB, M], BF16, name="w1_raw", align_bytes=64)
-        w1_grp = keep.tile([P, M, JB], BF16, name="w1_grp", align_bytes=64)
+        w1_raw = keep.tile([P, PACK, M], BF16, name="w1_raw", align_bytes=64)
+        w1_grp = keep.tile([P, M, PACK], BF16, name="w1_grp", align_bytes=64)
         w1_codes = keep.tile([P, M], U32, name="w1_codes", align_bytes=64)
         w1_scales = keep.tile([P, M], U8, name="w1_scales", align_bytes=64)
-        b_col = [keep.tile([P, 1], BF16, name="b_col%d" % h, align_bytes=64) for h in range(2)]
+        b_col = [keep.tile([P, 1], BF16, name="b_col%d" % h, align_bytes=64) for h in range(HALVES)]
         b_bc = keep.tile([P, 2, M], BF16, name="b_bc", align_bytes=64)
+
+        ctx.enter_context(tc.manual_schedule())
 
         def rows(x, c):
             return x[c * CHUNK : (c + 1) * CHUNK]
 
-        def load_q(c):
-            nc.sync.dma_start(out=q_raw[c][:], in_=rows(q, c).rearrange("(p j) k -> p (j k)", j=JB))
+        def load_blocks(raw, x, c, j0=0, j1=JB):
+            src = rows(x, c).rearrange("(p j) k -> p j k", j=JB)[:, j0:j1, :]
+            nc.sync.dma_start(out=raw[c][:, j0 * E : j1 * E], in_=src.rearrange("p j k -> p (j k)"))
 
-        def load_r(c):
-            nc.sync.dma_start(out=r_raw[c][:], in_=rows(rep_bytes, c).rearrange("(p j) k -> p (j k)", j=JB))
-
-        words = (Wq_words, Wk_words, Wv_words)
-        scales = (Wq_scales, Wk_scales, Wv_scales)
-
-        def load_w(i):
-            nc.sync.dma_start(out=w_raw[i][:], in_=words[i][0].rearrange("p n t -> p (n t)").bitcast(I32))
-
-        def load_part(c, j0, j1, raw, x):
-            nc.sync.dma_start(
-                out=raw[c][:, j0 * E : j1 * E],
-                in_=rows(x, c).rearrange("(p j) k -> p j k", j=JB)[:, j0:j1, :].rearrange("p j k -> p (j k)"),
-            )
+        def load_weight(i):
+            words = (Wq_words, Wk_words, Wv_words)[i]
+            nc.sync.dma_start(out=w_raw[i][:], in_=words[0].rearrange("p n t -> p (n t)").bitcast(I32))
 
         nc.vector.memset(ws_raw[:].bitcast(I32), 0)
-        nc.scalar.dma_start(out=scale_col[:], in_=rep_scale.rearrange("o (p t) -> p (o t)", t=4))
-        scale_bank = psum.tile([P, 4, P], F32, name="k_bank")
-        for t in range(4):
-            nc.tensor.transpose(scale_bank[:, t, :], scale_col[:, t : t + 1].to_broadcast([P, P]), ident[:])
-        nc.scalar.activation(out=warm[:], in_=warm[:], func=ACT.Sigmoid)
-        nc.scalar.copy(out=scale_bc[:].rearrange("p (n t) -> p n t", t=4), in_=scale_bank[:].rearrange("p t n -> p n t"))
-        for i in (1, 0, 2):
-            for quad in range(4):
-                lo = 32 * quad + 4 * i
+        nc.scalar.dma_start(out=scale_col[:], in_=rep_scale.rearrange("o (p t) -> p (o t)", t=PACK))
+        load_blocks(r_raw, rep_bytes, 0)
+        for i, scales in ((1, Wk_scales), (0, Wq_scales), (2, Wv_scales)):
+            for quadrant in range(4):
+                row = 32 * quadrant + 4 * i
                 nc.sync.dma_start(
-                    out=ws_raw[lo : lo + 4, :].bitcast(I32), in_=scales[i][0, 4 * quad : 4 * quad + 4, :].bitcast(I32)
+                    out=ws_raw[row : row + 4, :].bitcast(I32),
+                    in_=scales[0, 4 * quadrant : 4 * quadrant + 4, :].bitcast(I32),
                 )
-        load_r(0)
-        nc.sync.dma_start(out=w1_raw[:], in_=W1[0].rearrange("(p j) m -> p j m", j=JB))
-        load_part(0, 0, 2, q_raw, q)
-        load_w(1)
-        load_w(0)
-        load_part(0, 2, 4, q_raw, q)
-        load_w(2)
-        load_r(1)
-        load_q(1)
-        for c in range(2, CHUNKS):
-            load_r(c)
-            load_q(c)
+        nc.sync.dma_start(out=w1_raw[:], in_=W1[0].rearrange("(p t) m -> p t m", t=PACK))
+        load_blocks(q_raw, q, 0, 0, 2)
+        load_weight(1)
+        load_weight(0)
+        load_blocks(q_raw, q, 0, 2, JB)
+        load_weight(2)
+        for c in range(1, CHUNKS):
+            load_blocks(r_raw, rep_bytes, c)
+            load_blocks(q_raw, q, c)
             if c == 2:
                 with nc.allow_non_contiguous_dma(reason="one bias value to a partition, 256 in all"):
-                    for h in range(2):
+                    for h in range(HALVES):
                         nc.sync.dma_start(out=b_col[h][:], in_=b1[:, h * P : (h + 1) * P].rearrange("o p -> p o"))
         nc.sync.dma_start(out=b_bc[:, 0, :], in_=b1.rearrange("o m -> (o m)").partition_broadcast(P))
 
-        r_bf, r_bank, q_bank, r_grp, q_grp = {}, {}, {}, {}, {}
-        r_codes, r_scales, q_codes, q_scales = {}, {}, {}, {}
-        k_bank, q_acc, v_bank, k_sb, gate, z_grp, z_codes, z_scales = {}, {}, {}, {}, {}, {}, {}, {}
-        o_bank, o_sb, t_bank, res = {}, {}, {}, {}
+        scale_bank = psum.tile([P, PACK, P], F32, name="k_bank")
+        for t in range(PACK):
+            nc.tensor.transpose(scale_bank[:, t, :], scale_col[:, t : t + 1].to_broadcast([P, P]), ident[:])
+        nc.scalar.activation(out=warm[:], in_=warm[:], func=ACT.Sigmoid)
+        nc.scalar.copy(out=scale_bc[:].rearrange("p (n t) -> p n t", t=PACK), in_=scale_bank[:].rearrange("p t n -> p n t"))
+        nc.scalar.copy(out=w1_grp[:], in_=w1_raw[:].rearrange("p t m -> p m t"))
 
-        def permute_w(i):
+        r_bf, r_bank, q_bank, r_grp, q_grp, r_mx, q_mx = {}, {}, {}, {}, {}, {}, {}
+        k_bank, qp_bank, v_bank, k_sb, qk, gate, z_grp, z_mx = {}, {}, {}, {}, {}, {}, {}, {}
+        o_bank, o_sb, t_bank, res, token_bank, token_sum = {}, {}, {}, {}, {}, {}
+
+        def permute_columns(dst, src):
             nc.vector.tensor_copy(
-                out=w_codes[i][:].rearrange("p (t m) -> p t m", t=4), in_=w_raw[i][:].rearrange("p (m t) -> p t m", t=4)
+                out=dst[:].rearrange("p (t m) -> p t m", t=PACK), in_=src[:].rearrange("p (m t) -> p t m", t=PACK)
             )
 
-        def permute_scales():
-            nc.vector.tensor_copy(
-                out=ws[:].rearrange("p (t m) -> p t m", t=4), in_=ws_raw[:].rearrange("p (m t) -> p t m", t=4)
-            )
-
-        def prod(b):
-            if not 0 <= b < BLOCKS:
-                return
-            h, i = b // 2, b % 2
-            if i == 0:
-                r_bf[h] = stage.tile([P, 2 * E], BF16, name="r_bf", align_bytes=64)
+        def scale_rep(b):
+            if b % 2 == 0:
+                r_bf[b // 2] = stage.tile([P, 2 * E], BF16, name="r_bf", align_bytes=64)
             j = b % JB
             nc.vector.tensor_tensor(
-                out=r_bf[h][:, i * E : (i + 1) * E],
+                out=r_bf[b // 2][:, (b % 2) * E : (b % 2 + 1) * E],
                 in0=r_raw[b // JB][:, j * E : (j + 1) * E].bitcast(F8),
                 in1=scale_bc[:],
-                op=ALU.mult,
+                op=MULT,
             )
 
-        def transposes(b0):
-            if not 0 <= b0 < BLOCKS:
-                return
-            h = b0 // 2
-            r_bank[h] = psum.tile([P, 2, 2, P], F32, name="r_bank")
-            q_bank[h] = psum.tile([P, 2, 2, P], F32, name="q_bank")
-            rw = r_bf[h][:].bitcast(F32)
-            qw = q_raw[b0 // JB][:].bitcast(F32)
-            qoff = (b0 % JB) * (E // 2)
-            for bank, w, off in ((r_bank[h], rw, 0), (q_bank[h], qw, qoff)):
-                for i in range(2):
-                    for u in range(2):
-                        lo = off + i * (E // 2)
-                        nc.tensor.transpose(bank[:, i, u, :], w[:, lo + u : lo + E // 2 : 2], ident[:])
+        def transpose_block(bank, words, i, first):
+            for u in range(2):
+                nc.tensor.transpose(bank[:, i, u, :], words[:, first + u : first + WORDS : 2], ident[:])
 
-        def head_half():
-            r_bank[0] = psum.tile([P, 2, 2, P], F32, name="r_bank")
-            q_bank[0] = psum.tile([P, 2, 2, P], F32, name="q_bank")
-            qw = q_raw[0][:].bitcast(F32)
+        def transpose_q(pair):
+            q_bank[pair] = psum.tile([P, 2, 2, P], F32, name="q_bank")
             for i in range(2):
-                for u in range(2):
-                    lo = i * (E // 2)
-                    nc.tensor.transpose(q_bank[0][:, i, u, :], qw[:, lo + u : lo + E // 2 : 2], ident[:])
-            evac_q(0)
-            r_grp[0] = stage.tile([P, 2 * P * 4], BF16, name="r_grp", align_bytes=64)
-            r_codes[0] = stage.tile([P, 2 * P], U32, name="r_codes", align_bytes=64)
-            r_scales[0] = stage.tile([P, 2 * P], U8, name="r_scales", align_bytes=64)
-            for i in range(2):
-                prod(i)
-                rw = r_bf[0][:].bitcast(F32)
-                lo = i * (E // 2)
-                for u in range(2):
-                    nc.tensor.transpose(r_bank[0][:, i, u, :], rw[:, lo + u : lo + E // 2 : 2], ident[:])
-                nc.scalar.copy(
-                    out=r_grp[0][:, i * E : (i + 1) * E].bitcast(F32).rearrange("p (r u) -> p r u", u=2),
-                    in_=r_bank[0][:, i].rearrange("p u r -> p r u"),
-                )
-            permute_scales()
-            permute_w(1)
-            prod(2)
-            for i in range(2):
-                nc.vector.quantize_mx(
-                    out=r_codes[0][:, i * P : (i + 1) * P].bitcast(FP8X4),
-                    scales=r_scales[0][:, i * P : (i + 1) * P],
-                    in_=r_grp[0][:, i * E : (i + 1) * E],
-                )
-                if i == 0:
-                    quant_q(0)
-                    permute_w(0)
-                    prod(3)
-            mm_k(0)
-            mm_q(0)
+                b = 2 * pair + i
+                transpose_block(q_bank[pair], q_raw[b // JB][:].bitcast(F32), i, (b % JB) * WORDS)
 
-        def evac(bank, tag):
-            grp = stage.tile([P, 2 * P * 4], BF16, name=tag, align_bytes=64)
+        def transpose_pair(pair):
+            r_bank[pair] = psum.tile([P, 2, 2, P], F32, name="r_bank")
+            for i in range(2):
+                transpose_block(r_bank[pair], r_bf[pair][:].bitcast(F32), i, i * WORDS)
+            transpose_q(pair)
+
+        def empty_bank(bank, name):
+            grouped = stage.tile([P, 2 * P * PACK], BF16, name=name, align_bytes=64)
             nc.scalar.copy(
-                out=grp[:].bitcast(F32).rearrange("p (i r u) -> p i r u", i=2, u=2),
+                out=grouped[:].bitcast(F32).rearrange("p (i r u) -> p i r u", i=2, u=2),
                 in_=bank[:].rearrange("p i u r -> p i r u"),
             )
-            return grp
+            return grouped
 
-        def evac_r(b0):
-            if 0 <= b0 < BLOCKS:
-                r_grp[b0 // 2] = evac(r_bank[b0 // 2], "r_grp")
+        def empty_r(pair):
+            r_grp[pair] = empty_bank(r_bank[pair], "r_grp")
 
-        def evac_q(b0):
-            if 0 <= b0 < BLOCKS:
-                q_grp[b0 // 2] = evac(q_bank[b0 // 2], "q_grp")
+        def empty_q(pair):
+            q_grp[pair] = empty_bank(q_bank[pair], "q_grp")
 
-        def quant(grp, cols, tag):
-            codes = stage.tile([P, cols], U32, name=tag + "_codes", align_bytes=64)
-            sc = stage.tile([P, cols], U8, name=tag + "_scales", align_bytes=64)
-            nc.vector.quantize_mx(out=codes[:].bitcast(FP8X4), scales=sc[:], in_=grp)
-            return codes, sc
+        def mx_tiles(cols, name):
+            codes = stage.tile([P, cols], U32, name=name + "_codes", align_bytes=64)
+            return codes, stage.tile([P, cols], U8, name=name + "_scales", align_bytes=64)
 
-        def quant_r(b0):
-            if 0 <= b0 < BLOCKS:
-                h = b0 // 2
-                r_codes[h], r_scales[h] = quant(r_grp[h][:], 2 * P, "r")
+        def quantise(grouped, cols, name):
+            codes, scales = mx_tiles(cols, name)
+            nc.vector.quantize_mx(out=codes[:].bitcast(FP8X4), scales=scales[:], in_=grouped)
+            return codes, scales
 
-        def quant_q(b0):
-            if 0 <= b0 < BLOCKS:
-                h = b0 // 2
-                q_codes[h], q_scales[h] = quant(q_grp[h][:], 2 * P, "q")
+        def quantise_r(pair):
+            r_mx[pair] = quantise(r_grp[pair][:], 2 * P, "r")
 
-        def project(bank, i, codes, sc, b):
-            cols = slice((b % 2) * P, (b % 2 + 1) * P)
-            for t in range(4):
-                wc = slice(t * P, (t + 1) * P)
+        def quantise_q(pair):
+            q_mx[pair] = quantise(q_grp[pair][:], 2 * P, "q")
+
+        def project(bank, i, mx, b):
+            codes, scales = mx[b // 2]
+            tokens = slice((b % 2) * P, (b % 2 + 1) * P)
+            for t in range(PACK):
+                features = slice(t * P, (t + 1) * P)
                 nc.tensor.matmul_mx(
                     out=bank[:, t, :],
-                    lhsT=w_codes[i][:, wc].bitcast(FP8X4),
-                    lhsT_scale=ws[4 * i : P, wc],
-                    rhs=codes[:, cols].bitcast(FP8X4),
-                    rhs_scale=sc[:, cols],
+                    lhsT=w_codes[i][:, features].bitcast(FP8X4),
+                    lhsT_scale=ws[4 * i : P, features],
+                    rhs=codes[:, tokens].bitcast(FP8X4),
+                    rhs_scale=scales[:, tokens],
                     start=True,
                     stop=True,
                 )
 
-        def mm_q(b):
-            if 0 <= b < BLOCKS:
-                q_acc[b] = psum.tile([P, 4, P], F32, name="q_acc")
-                project(q_acc[b], 0, q_codes[b // 2], q_scales[b // 2], b)
+        def project_q(b):
+            qp_bank[b] = psum.tile([P, PACK, P], F32, name="qp_bank")
+            project(qp_bank[b], 0, q_mx, b)
 
-        def mm_k(b):
-            if 0 <= b < BLOCKS:
-                k_bank[b] = psum.tile([P, 4, P], F32, name="k_bank")
-                project(k_bank[b], 1, r_codes[b // 2], r_scales[b // 2], b)
+        def project_k(b):
+            k_bank[b] = psum.tile([P, PACK, P], F32, name="k_bank")
+            project(k_bank[b], 1, r_mx, b)
 
-        def mm_v(b):
-            if 0 <= b < BLOCKS:
-                v_bank[b] = psum.tile([P, 4, P], F32, name="v_bank", bufs=2)
-                project(v_bank[b], 2, r_codes[b // 2], r_scales[b // 2], b)
+        def project_v(b):
+            v_bank[b] = psum.tile([P, PACK, P], F32, name="v_bank", bufs=2)
+            project(v_bank[b], 2, r_mx, b)
 
         def copy_k(b):
-            if 0 <= b < BLOCKS:
-                k_sb[b] = stage.tile([P, P, 4], F32, name="k_sb", align_bytes=64)
-                nc.scalar.copy(out=k_sb[b][:], in_=k_bank[b][:].rearrange("p t n -> p n t"))
+            k_sb[b] = stage.tile([P, P, PACK], F32, name="k_sb", align_bytes=64)
+            nc.scalar.copy(out=k_sb[b][:], in_=k_bank[b][:].rearrange("p t n -> p n t"))
 
-        def mul_qk(b):
-            if 0 <= b < BLOCKS:
-                gate[b] = stage.tile([P, P, 4], F32, name="gate", align_bytes=64)
-                nc.vector.tensor_tensor(
-                    out=gate[b][:], in0=q_acc[b][:].rearrange("p t n -> p n t"), in1=k_sb[b][:], op=ALU.mult
-                )
-
-        def sigmoid(b):
-            if 0 <= b < BLOCKS:
-                k_sb[b] = stage.tile([P, P, 4], F32, name="sig", align_bytes=64)
-                nc.scalar.activation(out=k_sb[b][:], in_=gate[b][:], func=ACT.Sigmoid, scale=GATE_SCALE)
-
-        def mul_v(b):
-            if 0 <= b < BLOCKS:
-                c, j = b // JB, b % JB
-                if j == 0:
-                    z_grp[c] = stage.tile([P, CHUNK, 4], BF16, name="z_grp", align_bytes=64, bufs=2)
-                nc.vector.tensor_tensor(
-                    out=z_grp[c][:, j * P : (j + 1) * P, :],
-                    in0=v_bank[b][:].rearrange("p t n -> p n t"),
-                    in1=k_sb[b][:],
-                    op=ALU.mult,
-                )
-
-        def quant_z(c):
-            if 0 <= c < E2_CHUNKS:
-                z_codes[c], z_scales[c] = quant(z_grp[c][:].rearrange("p n t -> p (n t)"), CHUNK, "z")
-
-        def layer(c):
-            if 0 <= c < E2_CHUNKS:
-                for h in range(2):
-                    o_bank[c, h] = psum.tile([P, CHUNK], F32, name="o_bank%d" % h)
-                    wc = slice(h * P, (h + 1) * P)
-                    nc.tensor.matmul_mx(
-                        out=o_bank[c, h][:],
-                        lhsT=w1_codes[:, wc].bitcast(FP8X4),
-                        lhsT_scale=w1_scales[:, wc],
-                        rhs=z_codes[c][:].bitcast(FP8X4),
-                        rhs_scale=z_scales[c][:],
-                        start=True,
-                        stop=True,
-                    )
-
-        def relu(c, h):
-            if 0 <= c < E2_CHUNKS:
-                o_sb[c, h] = stage.tile([P, CHUNK], F32, name="o_sb%d" % h, align_bytes=64, bufs=2)
-                nc.scalar.activation(
-                    out=o_sb[c, h][:], in_=o_bank[c, h][:], func=ACT.Relu, bias=b_col[h][:]
-                )
-
-        def turn(c):
-            if 0 <= c < E2_CHUNKS:
-                for half in range(2):
-                    t_bank[c, half] = psum.tile([P, 2, M], F32, name="o_bank%d" % half)
-                    for jj in range(2):
-                        j = 2 * half + jj
-                        for h in range(2):
-                            nc.tensor.transpose(
-                                t_bank[c, half][:, jj, h * P : (h + 1) * P], o_sb[c, h][:, j * P : (j + 1) * P], ident[:]
-                            )
-
-        def finish(c, half):
-            if 0 <= c < E2_CHUNKS:
-                if half == 0:
-                    res[c] = stage.tile([P, JB, M], F32, name="res", align_bytes=64, bufs=2)
-                nc.scalar.copy(out=res[c][:, 2 * half : 2 * half + 2, :], in_=t_bank[c, half][:])
-                if half == 1:
-                    nc.sync.dma_start(out=rows(out, c).rearrange("(p j) o m -> p j (o m)", j=JB), in_=res[c][:])
-
-        def tail_quant(b, n):
-            c, j = b // JB, b % JB
-            z_codes[b, 0], z_scales[b, 0] = quant(
-                z_grp[c][:, j * P : (j + n) * P, :].rearrange("p n t -> p (n t)"), n * P, "zl%d" % n
+        def multiply_qk(b):
+            qk[b] = stage.tile([P, P, PACK], F32, name="qk", align_bytes=64)
+            nc.vector.tensor_tensor(
+                out=qk[b][:], in0=qp_bank[b][:].rearrange("p t n -> p n t"), in1=k_sb[b][:], op=MULT
             )
 
-        def tail_layer(b, n, tag):
-            o_bank[b, 2] = psum.tile([P, n, M], F32, name=tag)
-            for i in range(n):
-                cols = slice(i * P, (i + 1) * P)
+        def sigmoid(b):
+            gate[b] = stage.tile([P, P, PACK], F32, name="gate", align_bytes=64)
+            nc.scalar.activation(out=gate[b][:], in_=qk[b][:], func=ACT.Sigmoid, scale=GATE_SCALE)
+
+        def multiply_v(b):
+            c, j = b // JB, b % JB
+            if j == 0:
+                z_grp[c] = stage.tile([P, CHUNK, PACK], BF16, name="z_grp", align_bytes=64, bufs=2)
+            nc.vector.tensor_tensor(
+                out=z_grp[c][:, j * P : (j + 1) * P, :],
+                in0=v_bank[b][:].rearrange("p t n -> p n t"),
+                in1=gate[b][:],
+                op=MULT,
+            )
+
+        def quantise_z(c):
+            z_mx[c] = quantise(z_grp[c][:].rearrange("p n t -> p (n t)"), CHUNK, "z")
+
+        def layer(c):
+            codes, scales = z_mx[c]
+            for h in range(HALVES):
+                channels = slice(h * P, (h + 1) * P)
+                o_bank[c, h] = psum.tile([P, CHUNK], F32, name="o_bank%d" % h)
                 nc.tensor.matmul_mx(
-                    out=o_bank[b, 2][:, i, :],
-                    lhsT=z_codes[b, 0][:, cols].bitcast(FP8X4),
-                    lhsT_scale=z_scales[b, 0][:, cols],
+                    out=o_bank[c, h][:],
+                    lhsT=w1_codes[:, channels].bitcast(FP8X4),
+                    lhsT_scale=w1_scales[:, channels],
+                    rhs=codes[:].bitcast(FP8X4),
+                    rhs_scale=scales[:],
+                    start=True,
+                    stop=True,
+                )
+
+        def bias_relu(c, h):
+            o_sb[c, h] = stage.tile([P, CHUNK], F32, name="o_sb%d" % h, align_bytes=64, bufs=2)
+            nc.scalar.activation(out=o_sb[c, h][:], in_=o_bank[c, h][:], func=ACT.Relu, bias=b_col[h][:])
+
+        def turn(c):
+            for half in range(2):
+                t_bank[c, half] = psum.tile([P, 2, M], F32, name="o_bank%d" % half)
+                for i in range(2):
+                    tokens = slice((2 * half + i) * P, (2 * half + i + 1) * P)
+                    for h in range(HALVES):
+                        nc.tensor.transpose(
+                            t_bank[c, half][:, i, h * P : (h + 1) * P], o_sb[c, h][:, tokens], ident[:]
+                        )
+
+        def store_blocks(x, c, j0, j1):
+            dst = rows(out, c).rearrange("(p j) o m -> p j (o m)", j=JB)
+            nc.sync.dma_start(out=dst[:, j0:j1, :], in_=x[:])
+
+        def finish(c, half):
+            if half == 0:
+                res[c] = stage.tile([P, JB, M], F32, name="res", align_bytes=64, bufs=2)
+            nc.scalar.copy(out=res[c][:, 2 * half : 2 * half + 2, :], in_=t_bank[c, half][:])
+            if half == 1:
+                store_blocks(res[c], c, 0, JB)
+
+        def token_quantise(b, n):
+            c, j = b // JB, b % JB
+            z = z_grp[c][:, j * P : (j + n) * P, :]
+            z_mx["tokens", b] = quantise(z.rearrange("p n t -> p (n t)"), n * P, "zt%d" % n)
+
+        def token_layer(b, n, bank):
+            codes, scales = z_mx["tokens", b]
+            token_bank[b] = psum.tile([P, n, M], F32, name=bank)
+            for i in range(n):
+                tokens = slice(i * P, (i + 1) * P)
+                nc.tensor.matmul_mx(
+                    out=token_bank[b][:, i, :],
+                    lhsT=codes[:, tokens].bitcast(FP8X4),
+                    lhsT_scale=scales[:, tokens],
                     rhs=w1_codes[:].bitcast(FP8X4),
                     rhs_scale=w1_scales[:],
                     start=True,
                     stop=True,
                 )
 
-        def tail_add(b, n):
-            res[b, 0] = stage.tile([P, n, M], F32, name="pre%d" % n, align_bytes=64)
-            nc.vector.tensor_tensor(out=res[b, 0][:], in0=o_bank[b, 2][:], in1=b_bc[:, 0:n, :], op=ALU.add)
+        def token_bias(b, n):
+            token_sum[b] = stage.tile([P, n, M], F32, name="token_sum%d" % n, align_bytes=64)
+            nc.vector.tensor_tensor(out=token_sum[b][:], in0=token_bank[b][:], in1=b_bc[:, 0:n, :], op=ADD)
 
-        def tail_relu(b, n):
-            res[b, 1] = stage.tile([P, n, M], F32, name="post%d" % n, align_bytes=64)
-            nc.scalar.activation(out=res[b, 1][:], in_=res[b, 0][:], func=ACT.Relu)
-            j = b % JB
-            nc.sync.dma_start(
-                out=rows(out, b // JB).rearrange("(p j) o m -> p j (o m)", j=JB)[:, j : j + n, :], in_=res[b, 1][:]
+        def token_finish(b, n):
+            done = stage.tile([P, n, M], F32, name="token_out%d" % n, align_bytes=64)
+            nc.scalar.activation(out=done[:], in_=token_sum[b][:], func=ACT.Relu)
+            store_blocks(done, b // JB, b % JB, b % JB + n)
+
+        transpose_q(0)
+        empty_q(0)
+        r_bank[0] = psum.tile([P, 2, 2, P], F32, name="r_bank")
+        r_grp[0] = stage.tile([P, 2 * P * PACK], BF16, name="r_grp", align_bytes=64)
+        r_mx[0] = mx_tiles(2 * P, "r")
+        for b in range(2):
+            scale_rep(b)
+            transpose_block(r_bank[0], r_bf[0][:].bitcast(F32), b, b * WORDS)
+            nc.scalar.copy(
+                out=r_grp[0][:, b * E : (b + 1) * E].bitcast(F32).rearrange("p (r u) -> p r u", u=2),
+                in_=r_bank[0][:, b].rearrange("p u r -> p r u"),
             )
+        permute_columns(ws, ws_raw)
+        permute_columns(w_codes[1], w_raw[1])
+        scale_rep(2)
+        for b in range(2):
+            tokens = slice(b * P, (b + 1) * P)
+            nc.vector.quantize_mx(
+                out=r_mx[0][0][:, tokens].bitcast(FP8X4), scales=r_mx[0][1][:, tokens], in_=r_grp[0][:, b * E : (b + 1) * E]
+            )
+            if b == 0:
+                quantise_q(0)
+                permute_columns(w_codes[0], w_raw[0])
+                scale_rep(3)
+        project_k(0)
+        project_q(0)
 
-        nc.scalar.copy(out=w1_grp[:], in_=w1_raw[:].rearrange("p j m -> p m j"))
-        head_half()
-        for s in range(-1, BLOCKS + 3):
-            m4 = s % 4
-            even = s % 2 == 0
-            mm_v(s)
-            mul_qk(s)
-            copy_k(s + 1)
-            if not even:
-                transposes(s + 3)
-            if m4 == 2:
-                layer((s - 6) // 4)
-            if m4 == 0:
-                turn((s - 8) // 4)
-            if s == 27:
-                tail_quant(24, 2)
-            if s == 29:
-                tail_quant(26, 2)
-                tail_layer(26, 2, "q_bank")
-                tail_add(24, 2)
-            if s == 31:
-                tail_quant(28, 2)
-                tail_layer(28, 2, "r_bank")
-            if s == 32:
-                tail_add(28, 2)
-            if even:
-                quant_r(s + 2)
+        def call(stage_of, n, count, *args):
+            if 0 <= n < count:
+                stage_of(n, *args)
+
+        def chunk(behind):
+            return (s - behind) // JB if (s - behind) % JB == 0 else -1
+
+        for s in range(-1, BLOCKS + 2):
+            early = (s + 3) // 2 if s % 2 else (s + 2) // 2
+            for b, bank, s_quantise, s_layer, s_bias, s_finish in TOKEN_PAIRS:
+                if s == s_quantise:
+                    token_quantise(b, 2)
+                if s == s_layer:
+                    token_layer(b, 2, bank)
+                if s == s_bias:
+                    token_bias(b, 2)
+                if s == s_finish:
+                    token_finish(b, 2)
+            if s % 2:
+                call(transpose_pair, early, BLOCKS // 2)
+                call(multiply_qk, s, BLOCKS)
+                call(copy_k, s + 1, BLOCKS)
+                call(bias_relu, chunk(7), CHANNEL_CHUNKS, 1)
+                call(finish, chunk(9), CHANNEL_CHUNKS, 1)
+                call(empty_r, early, BLOCKS // 2)
+                call(multiply_v, s - 1, BLOCKS)
+                call(quantise_z, chunk(5), CHANNEL_CHUNKS)
+                if s > 0:
+                    call(scale_rep, s + 5, BLOCKS)
+                else:
+                    permute_columns(w_codes[2], w_raw[2])
+                call(sigmoid, s, BLOCKS)
+                if s > 0:
+                    call(project_q, s + 1, BLOCKS)
+                call(project_k, s + 2, BLOCKS)
+                call(project_v, s, BLOCKS)
             else:
-                if m4 == 1:
-                    quant_z((s - 5) // 4)
-                if s > -1:
-                    prod(s + 5)
-            if even:
-                evac_q(s + 2)
-            elif m4 == 3:
-                relu((s - 7) // 4, 1)
-            else:
-                finish((s - 9) // 4, 1)
-            if s == 28:
-                tail_layer(24, 2, "r_bank")
-            if s == 30:
-                tail_relu(24, 2)
-                tail_add(26, 2)
-            if s == 31:
-                tail_relu(26, 2)
-            mul_v(s - 1)
-            sigmoid(s)
-            if s == 32:
-                tail_relu(28, 2)
-            if s in (31, 32):
-                tail_quant(s - 1, 1)
-                tail_layer(s - 1, 1, "o_bank%d" % (s % 2))
-            if s in (32, 33):
-                tail_add(s - 2, 1)
-                tail_relu(s - 2, 1)
-            if even:
+                call(project_v, s, BLOCKS)
                 if s == 0:
-                    prod(4)
-                prod(s + 5)
-                quant_q(s + 2)
-            if s == -1:
-                permute_w(2)
-            if s == 25:
-                nc.scalar.copy(out=b_bc[:, 1, :], in_=b_bc[:, 0, :])
+                    scale_rep(4)
+                call(multiply_qk, s, BLOCKS)
+                call(empty_q, early, BLOCKS // 2)
+                call(turn, chunk(8), CHANNEL_CHUNKS)
+                call(layer, chunk(6), CHANNEL_CHUNKS)
+                call(quantise_r, early, BLOCKS // 2)
+                call(multiply_v, s - 1, BLOCKS)
+                call(copy_k, s + 1, BLOCKS)
+                call(scale_rep, s + 5, BLOCKS)
+                call(quantise_q, early, BLOCKS // 2)
+                call(bias_relu, chunk(6), CHANNEL_CHUNKS, 0)
+                call(sigmoid, s, BLOCKS)
+                call(finish, chunk(8), CHANNEL_CHUNKS, 0)
+                call(project_q, s + 1, BLOCKS)
+                call(project_k, s + 2, BLOCKS)
             if s == 4:
                 nc.vector.quantize_mx(
-                    out=w1_codes[:].bitcast(FP8X4), scales=w1_scales[:], in_=w1_grp[:].rearrange("p m j -> p (m j)")
+                    out=w1_codes[:].bitcast(FP8X4), scales=w1_scales[:], in_=w1_grp[:].rearrange("p m t -> p (m t)")
                 )
-            if not even:
-                evac_r(s + 3)
-            elif m4 == 2:
-                relu((s - 6) // 4, 0)
-            else:
-                finish((s - 8) // 4, 0)
-            if s > -1:
-                mm_q(s + 1)
-            mm_k(s + 2)
+            if s == TOKEN_BLOCK:
+                nc.scalar.copy(out=b_bc[:, 1, :], in_=b_bc[:, 0, :])
+            for b in (BLOCKS - 2, BLOCKS - 1):
+                if s == b + 1:
+                    token_quantise(b, 1)
+                    token_layer(b, 1, "o_bank%d" % (b % 2))
+                if s == b + 2:
+                    token_bias(b, 1)
+                    token_finish(b, 1)

@@ -81,7 +81,8 @@ def tile_treehopnode_pa_t_w8_kernel(
 
         nc.vector.memset(ws_raw[:].bitcast(I32), 0)
         nc.scalar.dma_start(out=scale_col[:], in_=rep_scale.rearrange("o (p t) -> p (o t)", t=PACK))
-        load_blocks(r_raw, rep_bytes, 0)
+        load_blocks(r_raw, rep_bytes, 0, 0, 2)
+        load_weight(1)
         for i, scales in ((1, Wk_scales), (0, Wq_scales), (2, Wv_scales)):
             for quadrant in range(4):
                 row = 32 * quadrant + 4 * i
@@ -89,14 +90,15 @@ def tile_treehopnode_pa_t_w8_kernel(
                     out=ws_raw[row : row + 4, :].bitcast(I32),
                     in_=scales[0, 4 * quadrant : 4 * quadrant + 4, :].bitcast(I32),
                 )
-        nc.sync.dma_start(out=w1_raw[:], in_=W1[0].rearrange("(p t) m -> p t m", t=PACK))
         load_blocks(q_raw, q, 0, 0, 2)
-        load_weight(1)
+        load_blocks(r_raw, rep_bytes, 0, 2, JB)
         load_weight(0)
         load_blocks(q_raw, q, 0, 2, JB)
-        load_weight(2)
         for c in range(1, CHUNKS):
             load_blocks(r_raw, rep_bytes, c)
+            if c == 1:
+                load_weight(2)
+                nc.sync.dma_start(out=w1_raw[:], in_=W1[0].rearrange("(p t) m -> p t m", t=PACK))
             load_blocks(q_raw, q, c)
             if c == 2:
                 with nc.allow_non_contiguous_dma(reason="one bias value to a partition, 256 in all"):
@@ -108,8 +110,11 @@ def tile_treehopnode_pa_t_w8_kernel(
         for t in range(PACK):
             nc.tensor.transpose(scale_bank[:, t, :], scale_col[:, t : t + 1].to_broadcast([P, P]), ident[:])
         nc.scalar.activation(out=warm[:], in_=warm[:], func=ACT.Sigmoid)
-        nc.scalar.copy(out=scale_bc[:].rearrange("p (n t) -> p n t", t=PACK), in_=scale_bank[:].rearrange("p t n -> p n t"))
-        nc.scalar.copy(out=w1_grp[:], in_=w1_raw[:].rearrange("p t m -> p m t"))
+
+        def spread_scale():
+            nc.scalar.copy(
+                out=scale_bc[:].rearrange("p (n t) -> p n t", t=PACK), in_=scale_bank[:].rearrange("p t n -> p n t")
+            )
 
         r_bf, r_bank, q_bank, r_grp, q_grp, r_mx, q_mx = {}, {}, {}, {}, {}, {}, {}
         k_bank, qp_bank, v_bank, k_sb, qk, gate, z_grp, z_mx = {}, {}, {}, {}, {}, {}, {}, {}
@@ -300,32 +305,43 @@ def tile_treehopnode_pa_t_w8_kernel(
             nc.scalar.activation(out=done[:], in_=token_sum[b][:], func=ACT.Relu)
             store_blocks(done, b // JB, b % JB, b % JB + n)
 
-        transpose_q(0)
-        empty_q(0)
+        r_bf[0] = stage.tile([P, 2 * E], BF16, name="r_bf", align_bytes=64)
         r_bank[0] = psum.tile([P, 2, 2, P], F32, name="r_bank")
         r_grp[0] = stage.tile([P, 2 * P * PACK], BF16, name="r_grp", align_bytes=64)
         r_mx[0] = mx_tiles(2 * P, "r")
         for b in range(2):
-            scale_rep(b)
+            nc.scalar.copy(out=r_bf[0][:, b * E : (b + 1) * E], in_=r_raw[0][:, b * E : (b + 1) * E].bitcast(F8))
             transpose_block(r_bank[0], r_bf[0][:].bitcast(F32), b, b * WORDS)
-            nc.scalar.copy(
-                out=r_grp[0][:, b * E : (b + 1) * E].bitcast(F32).rearrange("p (r u) -> p r u", u=2),
-                in_=r_bank[0][:, b].rearrange("p u r -> p r u"),
-            )
-        permute_columns(ws, ws_raw)
+        spread_scale()
         permute_columns(w_codes[1], w_raw[1])
+        for b in range(2):
+            nc.vector.tensor_tensor(
+                out=r_grp[0][:, b * E : (b + 1) * E].rearrange("p (n u e) -> p n u e", u=2, e=2),
+                in0=r_bank[0][:, b].bitcast(BF16).rearrange("p u (n e) -> p n u e", e=2),
+                in1=scale_col[:].rearrange("p (o u e) -> p o u e", o=1, u=2).to_broadcast([P, P, 2, 2]),
+                op=MULT,
+            )
+            if b == 0:
+                permute_columns(ws, ws_raw)
+        transpose_q(0)
+        empty_q(0)
         scale_rep(2)
         for b in range(2):
             tokens = slice(b * P, (b + 1) * P)
             nc.vector.quantize_mx(
                 out=r_mx[0][0][:, tokens].bitcast(FP8X4), scales=r_mx[0][1][:, tokens], in_=r_grp[0][:, b * E : (b + 1) * E]
             )
-            if b == 0:
-                quantise_q(0)
-                permute_columns(w_codes[0], w_raw[0])
-                scale_rep(3)
         project_k(0)
+        copy_k(0)
+        permute_columns(w_codes[0], w_raw[0])
+        quantise_q(0)
         project_q(0)
+        scale_rep(3)
+        transpose_pair(1)
+        empty_r(1)
+        scale_rep(4)
+        permute_columns(w_codes[2], w_raw[2])
+        project_k(1)
 
         def call(stage_of, n, count, *args):
             if 0 <= n < count:
@@ -334,7 +350,7 @@ def tile_treehopnode_pa_t_w8_kernel(
         def chunk(behind):
             return (s - behind) // JB if (s - behind) % JB == 0 else -1
 
-        for s in range(-1, BLOCKS + 2):
+        for s in range(BLOCKS + 2):
             early = (s + 3) // 2 if s % 2 else (s + 2) // 2
             for b, bank, s_quantise, s_layer, s_bias, s_finish in TOKEN_PAIRS:
                 if s == s_quantise:
@@ -354,19 +370,13 @@ def tile_treehopnode_pa_t_w8_kernel(
                 call(empty_r, early, BLOCKS // 2)
                 call(multiply_v, s - 1, BLOCKS)
                 call(quantise_z, chunk(5), CHANNEL_CHUNKS)
-                if s > 0:
-                    call(scale_rep, s + 5, BLOCKS)
-                else:
-                    permute_columns(w_codes[2], w_raw[2])
+                call(scale_rep, s + 5, BLOCKS)
                 call(sigmoid, s, BLOCKS)
-                if s > 0:
-                    call(project_q, s + 1, BLOCKS)
+                call(project_q, s + 1, BLOCKS)
                 call(project_k, s + 2, BLOCKS)
                 call(project_v, s, BLOCKS)
             else:
                 call(project_v, s, BLOCKS)
-                if s == 0:
-                    scale_rep(4)
                 call(multiply_qk, s, BLOCKS)
                 call(empty_q, early, BLOCKS // 2)
                 call(turn, chunk(8), CHANNEL_CHUNKS)
@@ -381,6 +391,8 @@ def tile_treehopnode_pa_t_w8_kernel(
                 call(finish, chunk(8), CHANNEL_CHUNKS, 0)
                 call(project_q, s + 1, BLOCKS)
                 call(project_k, s + 2, BLOCKS)
+            if s == 2:
+                nc.scalar.copy(out=w1_grp[:], in_=w1_raw[:].rearrange("p t m -> p m t"))
             if s == 4:
                 nc.vector.quantize_mx(
                     out=w1_codes[:].bitcast(FP8X4), scales=w1_scales[:], in_=w1_grp[:].rearrange("p m t -> p (m t)")

from contextlib import ExitStack

import concourse.mybir as mybir
from concourse.masks import make_identity

N, E, G, M = 4096, 512, 512, 256
FLOPS = 2 * N * E * G * 3 + 2 * N * G * M

F32 = mybir.dt.float32
BF16 = mybir.dt.bfloat16
I32 = mybir.dt.int32
U32 = mybir.dt.uint32
U8 = mybir.dt.uint8
F8 = mybir.dt.float8_e4m3fn
FP8X4 = mybir.dt.float8_e4m3fn_x4
ACT = mybir.ActivationFunctionType
MULT = mybir.AluOpType.mult
ADD = mybir.AluOpType.add

P = 128
PACK = 4
WORDS = E // 2
CHUNK = 512
JB = CHUNK // P
BLOCKS = N // P
CHUNKS = N // CHUNK
HALVES = M // P
GATE_SCALE = 1.0 / G**0.5

CHANNEL_CHUNKS = CHUNKS - 2
TOKEN_BLOCK = CHANNEL_CHUNKS * JB

TOKEN_PAIRS = (
    (TOKEN_BLOCK, "r_bank", 27, 28, 29, 30),
    (TOKEN_BLOCK + 2, "q_bank", 29, 29, 30, 31),
    (TOKEN_BLOCK + 4, "r_bank", 31, 31, 32, 32),
)


def tile_treehopnode_pa_t_w8_kernel(
    tc, q, rep_bytes, rep_scale, Wq_words, Wq_scales, Wk_words, Wk_scales, Wv_words, Wv_scales, W1, b1, out
):
    nc = tc.nc
    with ExitStack() as ctx:
        keep = ctx.enter_context(tc.tile_pool(name="keep", bufs=1))
        stage = ctx.enter_context(tc.tile_pool(name="stage", bufs=3))
        psum = ctx.enter_context(tc.psum_pool(name="psum", bufs=1))

        ident = keep.tile([P, P], F32, name="ident", align_bytes=64)
        make_identity(nc, ident[:])
        warm = keep.tile([P, 1], F32, name="warm")
        nc.gpsimd.memset(warm[:], 0.0)

        q_raw = [keep.tile([P, JB * E], BF16, name="q_raw%d" % c, align_bytes=64) for c in range(CHUNKS)]
        r_raw = [keep.tile([P, JB * E], U8, name="r_raw%d" % c, align_bytes=64) for c in range(CHUNKS)]
        scale_col = keep.tile([P, PACK], F32, name="scale_col", align_bytes=64)
        scale_bc = keep.tile([P, E], F32, name="scale_bc", align_bytes=64)
        w_raw = [keep.tile([P, G], I32, name="w_raw%d" % i, align_bytes=64) for i in range(3)]
        w_codes = [keep.tile([P, G], I32, name="w_codes%d" % i, align_bytes=64) for i in range(3)]
        ws_raw = keep.tile([P, G], U8, name="ws_raw", align_bytes=64)
        ws = keep.tile([P, G], U8, name="ws", align_bytes=64)
        w1_raw = keep.tile([P, PACK, M], BF16, name="w1_raw", align_bytes=64)
        w1_grp = keep.tile([P, M, PACK], BF16, name="w1_grp", align_bytes=64)
        w1_codes = keep.tile([P, M], U32, name="w1_codes", align_bytes=64)
        w1_scales = keep.tile([P, M], U8, name="w1_scales", align_bytes=64)
        b_col = [keep.tile([P, 1], BF16, name="b_col%d" % h, align_bytes=64) for h in range(HALVES)]
        b_bc = keep.tile([P, 2, M], BF16, name="b_bc", align_bytes=64)

        ctx.enter_context(tc.manual_schedule())

        def rows(x, c):
            return x[c * CHUNK : (c + 1) * CHUNK]

        def load_blocks(raw, x, c, j0=0, j1=JB):
            src = rows(x, c).rearrange("(p j) k -> p j k", j=JB)[:, j0:j1, :]
            nc.sync.dma_start(out=raw[c][:, j0 * E : j1 * E], in_=src.rearrange("p j k -> p (j k)"))

        def load_weight(i):
            words = (Wq_words, Wk_words, Wv_words)[i]
            nc.sync.dma_start(out=w_raw[i][:], in_=words[0].rearrange("p n t -> p (n t)").bitcast(I32))

        nc.vector.memset(ws_raw[:].bitcast(I32), 0)
        nc.scalar.dma_start(out=scale_col[:], in_=rep_scale.rearrange("o (p t) -> p (o t)", t=PACK))
        load_blocks(r_raw, rep_bytes, 0, 0, 2)
        load_weight(1)
        for i, scales in ((1, Wk_scales), (0, Wq_scales), (2, Wv_scales)):
            for quadrant in range(4):
                row = 32 * quadrant + 4 * i
                nc.sync.dma_start(
                    out=ws_raw[row : row + 4, :].bitcast(I32),
                    in_=scales[0, 4 * quadrant : 4 * quadrant + 4, :].bitcast(I32),
                )
        load_blocks(q_raw, q, 0, 0, 2)
        load_blocks(r_raw, rep_bytes, 0, 2, JB)
        load_weight(0)
        load_blocks(q_raw, q, 0, 2, JB)
        for c in range(1, CHUNKS):
            load_blocks(r_raw, rep_bytes, c)
            if c == 1:
                load_weight(2)
                nc.sync.dma_start(out=w1_raw[:], in_=W1[0].rearrange("(p t) m -> p t m", t=PACK))
            load_blocks(q_raw, q, c)
            if c == 2:
                with nc.allow_non_contiguous_dma(reason="one bias value to a partition, 256 in all"):
                    for h in range(HALVES):
                        nc.sync.dma_start(out=b_col[h][:], in_=b1[:, h * P : (h + 1) * P].rearrange("o p -> p o"))
        nc.sync.dma_start(out=b_bc[:, 0, :], in_=b1.rearrange("o m -> (o m)").partition_broadcast(P))

        scale_bank = psum.tile([P, PACK, P], F32, name="k_bank")
        for t in range(PACK):
            nc.tensor.transpose(scale_bank[:, t, :], scale_col[:, t : t + 1].to_broadcast([P, P]), ident[:])
        nc.scalar.activation(out=warm[:], in_=warm[:], func=ACT.Sigmoid)

        def spread_scale():
            nc.scalar.copy(
                out=scale_bc[:].rearrange("p (n t) -> p n t", t=PACK), in_=scale_bank[:].rearrange("p t n -> p n t")
            )

        r_bf, r_bank, q_bank, r_grp, q_grp, r_mx, q_mx = {}, {}, {}, {}, {}, {}, {}
        k_bank, qp_bank, v_bank, k_sb, qk, gate, z_grp, z_mx = {}, {}, {}, {}, {}, {}, {}, {}
        o_bank, o_sb, t_bank, res, token_bank, token_sum = {}, {}, {}, {}, {}, {}

        def permute_columns(dst, src):
            nc.vector.tensor_copy(
                out=dst[:].rearrange("p (t m) -> p t m", t=PACK), in_=src[:].rearrange("p (m t) -> p t m", t=PACK)
            )

        def scale_rep(b):
            if b % 2 == 0:
                r_bf[b // 2] = stage.tile([P, 2 * E], BF16, name="r_bf", align_bytes=64)
            j = b % JB
            nc.vector.tensor_tensor(
                out=r_bf[b // 2][:, (b % 2) * E : (b % 2 + 1) * E],
                in0=r_raw[b // JB][:, j * E : (j + 1) * E].bitcast(F8),
                in1=scale_bc[:],
                op=MULT,
            )

        def transpose_block(bank, words, i, first):
            for u in range(2):
                nc.tensor.transpose(bank[:, i, u, :], words[:, first + u : first + WORDS : 2], ident[:])

        def transpose_q(pair):
            q_bank[pair] = psum.tile([P, 2, 2, P], F32, name="q_bank")
            for i in range(2):
                b = 2 * pair + i
                transpose_block(q_bank[pair], q_raw[b // JB][:].bitcast(F32), i, (b % JB) * WORDS)

        def transpose_pair(pair):
            r_bank[pair] = psum.tile([P, 2, 2, P], F32, name="r_bank")
            for i in range(2):
                transpose_block(r_bank[pair], r_bf[pair][:].bitcast(F32), i, i * WORDS)
            transpose_q(pair)

        def empty_bank(bank, name):
            grouped = stage.tile([P, 2 * P * PACK], BF16, name=name, align_bytes=64)
            nc.scalar.copy(
                out=grouped[:].bitcast(F32).rearrange("p (i r u) -> p i r u", i=2, u=2),
                in_=bank[:].rearrange("p i u r -> p i r u"),
            )
            return grouped

        def empty_r(pair):
            r_grp[pair] = empty_bank(r_bank[pair], "r_grp")

        def empty_q(pair):
            q_grp[pair] = empty_bank(q_bank[pair], "q_grp")

        def mx_tiles(cols, name):
            codes = stage.tile([P, cols], U32, name=name + "_codes", align_bytes=64)
            return codes, stage.tile([P, cols], U8, name=name + "_scales", align_bytes=64)

        def quantise(grouped, cols, name):
            codes, scales = mx_tiles(cols, name)
            nc.vector.quantize_mx(out=codes[:].bitcast(FP8X4), scales=scales[:], in_=grouped)
            return codes, scales

        def quantise_r(pair):
            r_mx[pair] = quantise(r_grp[pair][:], 2 * P, "r")

        def quantise_q(pair):
            q_mx[pair] = quantise(q_grp[pair][:], 2 * P, "q")

        def project(bank, i, mx, b):
            codes, scales = mx[b // 2]
            tokens = slice((b % 2) * P, (b % 2 + 1) * P)
            for t in range(PACK):
                features = slice(t * P, (t + 1) * P)
                nc.tensor.matmul_mx(
                    out=bank[:, t, :],
                    lhsT=w_codes[i][:, features].bitcast(FP8X4),
                    lhsT_scale=ws[4 * i : P, features],
                    rhs=codes[:, tokens].bitcast(FP8X4),
                    rhs_scale=scales[:, tokens],
                    start=True,
                    stop=True,
                )

        def project_q(b):
            qp_bank[b] = psum.tile([P, PACK, P], F32, name="qp_bank")
            project(qp_bank[b], 0, q_mx, b)

        def project_k(b):
            k_bank[b] = psum.tile([P, PACK, P], F32, name="k_bank")
            project(k_bank[b], 1, r_mx, b)

        def project_v(b):
            v_bank[b] = psum.tile([P, PACK, P], F32, name="v_bank", bufs=2)
            project(v_bank[b], 2, r_mx, b)

        def copy_k(b):
            k_sb[b] = stage.tile([P, P, PACK], F32, name="k_sb", align_bytes=64)
            nc.scalar.copy(out=k_sb[b][:], in_=k_bank[b][:].rearrange("p t n -> p n t"))

        def multiply_qk(b):
            qk[b] = stage.tile([P, P, PACK], F32, name="qk", align_bytes=64)
            nc.vector.tensor_tensor(
                out=qk[b][:], in0=qp_bank[b][:].rearrange("p t n -> p n t"), in1=k_sb[b][:], op=MULT
            )

        def sigmoid(b):
            gate[b] = stage.tile([P, P, PACK], F32, name="gate", align_bytes=64)
            nc.scalar.activation(out=gate[b][:], in_=qk[b][:], func=ACT.Sigmoid, scale=GATE_SCALE)

        def multiply_v(b):
            c, j = b // JB, b % JB
            if j == 0:
                z_grp[c] = stage.tile([P, CHUNK, PACK], BF16, name="z_grp", align_bytes=64, bufs=2)
            nc.vector.tensor_tensor(
                out=z_grp[c][:, j * P : (j + 1) * P, :],
                in0=v_bank[b][:].rearrange("p t n -> p n t"),
                in1=gate[b][:],
                op=MULT,
            )

        def quantise_z(c):
            z_mx[c] = quantise(z_grp[c][:].rearrange("p n t -> p (n t)"), CHUNK, "z")

        def layer(c):
            codes, scales = z_mx[c]
            for h in range(HALVES):
                channels = slice(h * P, (h + 1) * P)
                o_bank[c, h] = psum.tile([P, CHUNK], F32, name="o_bank%d" % h)
                nc.tensor.matmul_mx(
                    out=o_bank[c, h][:],
                    lhsT=w1_codes[:, channels].bitcast(FP8X4),
                    lhsT_scale=w1_scales[:, channels],
                    rhs=codes[:].bitcast(FP8X4),
                    rhs_scale=scales[:],
                    start=True,
                    stop=True,
                )

        def bias_relu(c, h):
            o_sb[c, h] = stage.tile([P, CHUNK], F32, name="o_sb%d" % h, align_bytes=64, bufs=2)
            nc.scalar.activation(out=o_sb[c, h][:], in_=o_bank[c, h][:], func=ACT.Relu, bias=b_col[h][:])

        def turn(c):
            for half in range(2):
                t_bank[c, half] = psum.tile([P, 2, M], F32, name="o_bank%d" % half)
                for i in range(2):
                    tokens = slice((2 * half + i) * P, (2 * half + i + 1) * P)
                    for h in range(HALVES):
                        nc.tensor.transpose(
                            t_bank[c, half][:, i, h * P : (h + 1) * P], o_sb[c, h][:, tokens], ident[:]
                        )

        def store_blocks(x, c, j0, j1):
            dst = rows(out, c).rearrange("(p j) o m -> p j (o m)", j=JB)
            nc.sync.dma_start(out=dst[:, j0:j1, :], in_=x[:])

        def finish(c, half):
            if half == 0:
                res[c] = stage.tile([P, JB, M], F32, name="res", align_bytes=64, bufs=2)
            nc.scalar.copy(out=res[c][:, 2 * half : 2 * half + 2, :], in_=t_bank[c, half][:])
            if half == 1:
                store_blocks(res[c], c, 0, JB)

        def token_quantise(b, n):
            c, j = b // JB, b % JB
            z = z_grp[c][:, j * P : (j + n) * P, :]
            z_mx["tokens", b] = quantise(z.rearrange("p n t -> p (n t)"), n * P, "zt%d" % n)

        def token_layer(b, n, bank):
            codes, scales = z_mx["tokens", b]
            token_bank[b] = psum.tile([P, n, M], F32, name=bank)
            for i in range(n):
                tokens = slice(i * P, (i + 1) * P)
                nc.tensor.matmul_mx(
                    out=token_bank[b][:, i, :],
                    lhsT=codes[:, tokens].bitcast(FP8X4),
                    lhsT_scale=scales[:, tokens],
                    rhs=w1_codes[:].bitcast(FP8X4),
                    rhs_scale=w1_scales[:],
                    start=True,
                    stop=True,
                )

        def token_bias(b, n):
            token_sum[b] = stage.tile([P, n, M], F32, name="token_sum%d" % n, align_bytes=64)
            nc.vector.tensor_tensor(out=token_sum[b][:], in0=token_bank[b][:], in1=b_bc[:, 0:n, :], op=ADD)

        def token_finish(b, n):
            done = stage.tile([P, n, M], F32, name="token_out%d" % n, align_bytes=64)
            nc.scalar.activation(out=done[:], in_=token_sum[b][:], func=ACT.Relu)
            store_blocks(done, b // JB, b % JB, b % JB + n)

        r_bf[0] = stage.tile([P, 2 * E], BF16, name="r_bf", align_bytes=64)
        r_bank[0] = psum.tile([P, 2, 2, P], F32, name="r_bank")
        r_grp[0] = stage.tile([P, 2 * P * PACK], BF16, name="r_grp", align_bytes=64)
        r_mx[0] = mx_tiles(2 * P, "r")
        for b in range(2):
            nc.scalar.copy(out=r_bf[0][:, b * E : (b + 1) * E], in_=r_raw[0][:, b * E : (b + 1) * E].bitcast(F8))
            transpose_block(r_bank[0], r_bf[0][:].bitcast(F32), b, b * WORDS)
        spread_scale()
        permute_columns(w_codes[1], w_raw[1])
        for b in range(2):
            nc.vector.tensor_tensor(
                out=r_grp[0][:, b * E : (b + 1) * E].rearrange("p (n u e) -> p n u e", u=2, e=2),
                in0=r_bank[0][:, b].bitcast(BF16).rearrange("p u (n e) -> p n u e", e=2),
                in1=scale_col[:].rearrange("p (o u e) -> p o u e", o=1, u=2).to_broadcast([P, P, 2, 2]),
                op=MULT,
            )
            if b == 0:
                permute_columns(ws, ws_raw)
        transpose_q(0)
        empty_q(0)
        scale_rep(2)
        for b in range(2):
            tokens = slice(b * P, (b + 1) * P)
            nc.vector.quantize_mx(
                out=r_mx[0][0][:, tokens].bitcast(FP8X4), scales=r_mx[0][1][:, tokens], in_=r_grp[0][:, b * E : (b + 1) * E]
            )
        project_k(0)
        copy_k(0)
        permute_columns(w_codes[0], w_raw[0])
        quantise_q(0)
        project_q(0)
        scale_rep(3)
        transpose_pair(1)
        empty_r(1)
        scale_rep(4)
        permute_columns(w_codes[2], w_raw[2])
        project_k(1)

        def call(stage_of, n, count, *args):
            if 0 <= n < count:
                stage_of(n, *args)

        def chunk(behind):
            return (s - behind) // JB if (s - behind) % JB == 0 else -1

        for s in range(BLOCKS + 2):
            early = (s + 3) // 2 if s % 2 else (s + 2) // 2
            for b, bank, s_quantise, s_layer, s_bias, s_finish in TOKEN_PAIRS:
                if s == s_quantise:
                    token_quantise(b, 2)
                if s == s_layer:
                    token_layer(b, 2, bank)
                if s == s_bias:
                    token_bias(b, 2)
                if s == s_finish:
                    token_finish(b, 2)
            if s % 2:
                call(transpose_pair, early, BLOCKS // 2)
                call(multiply_qk, s, BLOCKS)
                call(copy_k, s + 1, BLOCKS)
                call(bias_relu, chunk(7), CHANNEL_CHUNKS, 1)
                call(finish, chunk(9), CHANNEL_CHUNKS, 1)
                call(empty_r, early, BLOCKS // 2)
                call(multiply_v, s - 1, BLOCKS)
                call(quantise_z, chunk(5), CHANNEL_CHUNKS)
                call(scale_rep, s + 5, BLOCKS)
                call(sigmoid, s, BLOCKS)
                call(project_q, s + 1, BLOCKS)
                call(project_k, s + 2, BLOCKS)
                call(project_v, s, BLOCKS)
            else:
                call(project_v, s, BLOCKS)
                call(multiply_qk, s, BLOCKS)
                call(empty_q, early, BLOCKS // 2)
                call(turn, chunk(8), CHANNEL_CHUNKS)
                call(layer, chunk(6), CHANNEL_CHUNKS)
                call(quantise_r, early, BLOCKS // 2)
                call(multiply_v, s - 1, BLOCKS)
                call(copy_k, s + 1, BLOCKS)
                call(scale_rep, s + 5, BLOCKS)
                call(quantise_q, early, BLOCKS // 2)
                call(bias_relu, chunk(6), CHANNEL_CHUNKS, 0)
                call(sigmoid, s, BLOCKS)
                call(finish, chunk(8), CHANNEL_CHUNKS, 0)
                call(project_q, s + 1, BLOCKS)
                call(project_k, s + 2, BLOCKS)
            if s == 2:
                nc.scalar.copy(out=w1_grp[:], in_=w1_raw[:].rearrange("p t m -> p m t"))
            if s == 4:
                nc.vector.quantize_mx(
                    out=w1_codes[:].bitcast(FP8X4), scales=w1_scales[:], in_=w1_grp[:].rearrange("p m t -> p (m t)")
                )
            if s == TOKEN_BLOCK:
                nc.scalar.copy(out=b_bc[:, 1, :], in_=b_bc[:, 0, :])
            for b in (BLOCKS - 2, BLOCKS - 1):
                if s == b + 1:
                    token_quantise(b, 1)
                    token_layer(b, 1, "o_bank%d" % (b % 2))
                if s == b + 2:
                    token_bias(b, 1)
                    token_finish(b, 1)
